import numpy as np
import ml_dtypes


def mxq(x, axis, fmt="e4m3"):
    dtype, down = {"e4m3": (ml_dtypes.float8_e4m3fn, 7), "e5m2": (ml_dtypes.float8_e5m2, 14)}[fmt]
    v = np.moveaxis(np.asarray(x, np.float32).astype(ml_dtypes.bfloat16).astype(np.float64), axis, -1)
    blocks = v.reshape(v.shape[:-1] + (-1, 32))
    amax = np.abs(blocks).max(-1, keepdims=True)
    byte = np.maximum(np.where(amax > 0, np.frexp(amax)[1] - 1 + 127, 0) - down, 1)
    scale = np.exp2(byte - 127.0)
    codes = (blocks / scale).astype(np.float32).astype(dtype).astype(np.float64)
    return np.moveaxis((codes * scale).reshape(v.shape), -1, axis)


WIDE = False


def mx_kscale(k):
    if not WIDE:
        return np.ones(k)
    levels = np.array([10, -10, 5, -5, 0])
    a = np.random.permutation(np.resize(levels, k // 512 * 4)).reshape(k // 512, 4)
    idx = np.arange(k)
    return np.exp2(a[idx // 512, idx % 128 // 32])


BF16 = ml_dtypes.bfloat16


def bf(x):
    return np.asarray(x, np.float32).astype(BF16)


def f64(x):
    return np.asarray(x).astype(np.float64)


B, C, D, DV, H, W = 2, 128, 128, 512, 64, 64
N = H * W
M = (H // 2) * (W // 2)


def setup_inputs():
    t = mx_kscale(DV)
    return {"q": bf(np.random.standard_normal((B, N, D)) * 0.5),
            "k": bf((1.0 + 0.7 * np.random.standard_normal((B, D, M))) * 0.5),
            "v": bf((1.0 + 0.7 * np.random.standard_normal((B, DV, M))) * t[None, :, None]),
            "Wo": bf(np.random.standard_normal((C, DV)) / np.sqrt(DV) / t[None, :]),
            "gamma": bf(1.0 + 0.1 * np.random.standard_normal(1)),
            "x": bf(np.random.standard_normal((B, C, H, W)))}


def reference(q, k, v, Wo, gamma, x):
    s = f64(q) @ f64(k)
    e = np.exp(s - s.max(-1, keepdims=True))
    o = (mxq(f64(v), 2, "e4m3") @ mxq(e, 2, "e4m3").transpose(0, 2, 1)) / e.sum(-1)[:, None, :]
    y = mxq(f64(Wo), 1, "e4m3") @ mxq(o, 1, "e4m3")
    return (f64(gamma)[0] * y).reshape(B, C, H, W) + f64(x)

@@ -1,0 +1,318 @@
+from contextlib import ExitStack
+
+import concourse.mybir as mybir
+from concourse.masks import make_identity
+
+BF16 = mybir.dt.bfloat16
+F32 = mybir.dt.float32
+U32 = mybir.dt.uint32
+U8 = mybir.dt.uint8
+FP8X4 = mybir.dt.float8_e4m3fn_x4
+ALU = mybir.AluOpType
+ACT = mybir.ActivationFunctionType
+ALONG_FREE = mybir.AxisListType.X
+
+B, N, M, D, DV, C = 2, 4096, 1024, 128, 512, 128
+FLOPS = 2 * B * (N * D * M + DV * M * N + C * DV * N)
+
+P = 128
+PACK = 4
+PAIR = 2
+K_PASS = P * PACK
+BANK = 512
+HALVES = M // BANK
+E_PASSES = M // K_PASS
+TILES_PER_BATCH = N // P
+TILES = B * TILES_PER_BATCH
+GROUP = BANK // P
+GROUPS = TILES // GROUP
+Q_HEAD = 2 * GROUP
+V_CHUNKS = 4
+V_CHUNK_COLS = E_PASSES * DV // V_CHUNKS
+V_LATER_EVERY = 8
+
+
+def tile_selfattention_pb_t_kernel(tc, q, k, v, Wo, gamma, x, out):
+    nc = tc.nc
+    with ExitStack() as ctx:
+        ctx.enter_context(tc.manual_schedule())
+        keep = ctx.enter_context(tc.tile_pool(name="keep", bufs=1))
+        work = ctx.enter_context(tc.tile_pool(name="work", bufs=3))
+        psum = ctx.enter_context(tc.psum_pool(name="psum", bufs=1))
+
+        ident_bf16 = keep.tile([P, P], BF16)
+        make_identity(nc, ident_bf16[:])
+        ident_f32 = keep.tile([P, P], F32)
+        make_identity(nc, ident_f32[:])
+
+        k_sb = [keep.tile([P, M], BF16, name="k_sb%d" % b) for b in range(B)]
+        q_sb = [keep.tile([P, TILES_PER_BATCH, D], BF16, name="q_sb%d" % b) for b in range(B)]
+        v_sb = [keep.tile([P, (DV // P) * M], BF16, name="v_sb%d" % b) for b in range(B)]
+        x_sb = [keep.tile([P, N], BF16, name="x_sb%d" % b) for b in range(B)]
+        wo_sb = keep.tile([P, DV], BF16)
+        gamma_bf16 = keep.tile([P, 1], BF16)
+
+        q_rows = [q[b].rearrange("(t p) d -> p t d", p=P) for b in range(B)]
+        v_rows = [v[b].rearrange("(j p) m -> p j m", p=P) for b in range(B)]
+        x_cols = [x[b].rearrange("c h w -> c (h w)") for b in range(B)]
+        out_cols = [out[b].rearrange("c h w -> c (h w)") for b in range(B)]
+
+        nc.sync.dma_start(out=k_sb[0][:], in_=k[0])
+        nc.sync.dma_start(out=q_sb[0][:, 0:Q_HEAD, :], in_=q_rows[0][:, 0:Q_HEAD, :])
+        nc.sync.dma_start(out=wo_sb[:], in_=Wo)
+        nc.sync.dma_start(out=gamma_bf16[:], in_=gamma.partition_broadcast(P))
+        nc.sync.dma_start(out=v_sb[0][:].rearrange("p (j m) -> p j m", m=M), in_=v_rows[0])
+        nc.sync.dma_start(out=q_sb[0][:, Q_HEAD:, :], in_=q_rows[0][:, Q_HEAD:, :])
+        nc.sync.dma_start(out=v_sb[1][:].rearrange("p (j m) -> p j m", m=M), in_=v_rows[1])
+        nc.sync.dma_start(out=x_sb[0][:], in_=x_cols[0])
+        nc.sync.dma_start(out=k_sb[1][:], in_=k[1])
+        nc.sync.dma_start(out=q_sb[1][:], in_=q_rows[1])
+        nc.sync.dma_start(out=x_sb[1][:], in_=x_cols[1])
+
+        gamma_f32 = keep.tile([P, 1], F32)
+
+        v_grouped = [
+            keep.tile([P, E_PASSES * DV * PACK], BF16, name="v_grouped%d" % b, align_bytes=64)
+            for b in range(B)
+        ]
+        v_words = [keep.tile([P, E_PASSES * DV], U32, name="v_words%d" % b, align_bytes=64) for b in range(B)]
+        v_plane = [keep.tile([P, E_PASSES * DV], U8, name="v_plane%d" % b, align_bytes=64) for b in range(B)]
+        wo_grouped = keep.tile([P, C * PACK], BF16, align_bytes=64)
+        wo_words = keep.tile([P, C], U32, align_bytes=64)
+        wo_plane = keep.tile([P, C], U8, align_bytes=64)
+
+        q_cols, score_banks, half_maxima_of, neg_max, half_sums, recip = {}, {}, {}, {}, {}, {}
+        e_rows, e_grouped, e_words, e_plane = {}, {}, {}, {}
+        o_rows, o_grouped, o_words, o_plane = {}, {}, {}, {}
+
+        def quantise_wo():
+            wo_ps = psum.tile([P, PAIR, C], F32, tag="misc")
+            for u in range(PAIR):
+                nc.tensor.transpose(
+                    out=wo_ps[:, u, :], in_=wo_sb[:].bitcast(F32)[:, u * P : (u + 1) * P], identity=ident_f32[:]
+                )
+            nc.scalar.copy(
+                out=wo_grouped[:].bitcast(F32).rearrange("p (c u) -> p c u", u=PAIR),
+                in_=wo_ps[:].rearrange("p u c -> p c u"),
+            )
+            nc.vector.quantize_mx(out=wo_words[:].bitcast(FP8X4), scales=wo_plane[:], in_=wo_grouped[:])
+
+        def widen_gamma():
+            nc.vector.tensor_copy(out=gamma_f32[:], in_=gamma_bf16[:])
+
+        def transpose_v(b, chunk, copy_out):
+            g, h = divmod(chunk, PAIR)
+            v_ps = psum.tile([P, PAIR, PAIR, P], F32, tag="misc")
+            for j in range(PAIR):
+                for u in range(PAIR):
+                    first_word = (PAIR * h + j) * (M // PAIR) + (PAIR * g + u) * P
+                    nc.tensor.transpose(
+                        out=v_ps[:, j, u, :],
+                        in_=v_sb[b][:].bitcast(F32)[:, first_word : first_word + P],
+                        identity=ident_f32[:],
+                    )
+            copy_out(
+                out=v_grouped[b][:]
+                .bitcast(F32)
+                .rearrange("p (ch j c u) -> p ch j c u", ch=V_CHUNKS, j=PAIR, u=PAIR)[:, chunk],
+                in_=v_ps[:].rearrange("p j u c -> p j c u"),
+            )
+
+        def quantise_v(b, chunk):
+            cols = slice(chunk * V_CHUNK_COLS, (chunk + 1) * V_CHUNK_COLS)
+            nc.vector.quantize_mx(
+                out=v_words[b][:, cols].bitcast(FP8X4),
+                scales=v_plane[b][:, cols],
+                in_=v_grouped[b][:, chunk * V_CHUNK_COLS * PACK : (chunk + 1) * V_CHUNK_COLS * PACK],
+            )
+
+        def transpose_q(grp):
+            b, first = divmod(grp * GROUP, TILES_PER_BATCH)
+            q_ps = psum.tile([P, GROUP * P], BF16, tag="misc")
+            for i in range(GROUP):
+                nc.tensor.transpose(
+                    out=q_ps[:, i * P : (i + 1) * P], in_=q_sb[b][:, first + i, :], identity=ident_bf16[:]
+                )
+            q_t = work.tile([P, GROUP * P], BF16)
+            nc.vector.tensor_copy(out=q_t[:], in_=q_ps[:])
+            q_cols[grp] = q_t
+
+        def scores(t):
+            grp, i = divmod(t, GROUP)
+            banks = []
+            for h in range(HALVES):
+                bank = psum.tile([P, BANK], F32, tag="scores", bufs=2 * HALVES)
+                nc.tensor.matmul(
+                    out=bank[:],
+                    lhsT=q_cols[grp][:, i * P : (i + 1) * P],
+                    rhs=k_sb[t // TILES_PER_BATCH][:, h * BANK : (h + 1) * BANK],
+                    start=True,
+                    stop=True,
+                )
+                banks.append(bank)
+            score_banks[t] = banks
+
+        def half_maxima(t):
+            maxima = work.tile([P, HALVES], F32)
+            for h in range(HALVES):
+                nc.vector.tensor_reduce(
+                    out=maxima[:, h : h + 1], in_=score_banks[t][h][:], axis=ALONG_FREE, op=ALU.max
+                )
+            half_maxima_of[t] = maxima
+
+        def negated_maximum(t):
+            minus_max = work.tile([P, 1], F32)
+            nc.vector.tensor_reduce(
+                out=minus_max[:], in_=half_maxima_of[t][:], axis=ALONG_FREE, op=ALU.max, negate=True
+            )
+            neg_max[t] = minus_max
+
+        def exponentials(t):
+            grp, i = divmod(t, GROUP)
+            if i == 0:
+                half_sums[grp] = work.tile([P, GROUP, HALVES], F32, name="half_sum")
+            e_tile = work.tile([P, M], BF16)
+            for h in range(HALVES):
+                nc.scalar.activation(
+                    out=e_tile[:, h * BANK : (h + 1) * BANK],
+                    in_=score_banks[t][h][:],
+                    func=ACT.Exp,
+                    bias=neg_max[t][:, 0:1],
+                    scale=1.0,
+                    accum_out=half_sums[grp][:, i, h : h + 1],
+                )
+            e_rows[t] = e_tile
+
+        def reciprocal_sums(grp):
+            row_sum = work.tile([P, GROUP], F32)
+            nc.vector.tensor_reduce(out=row_sum[:], in_=half_sums[grp][:], axis=ALONG_FREE, op=ALU.add)
+            one_over = work.tile([P, GROUP], F32)
+            nc.vector.reciprocal(out=one_over[:], in_=row_sum[:])
+            recip[grp] = one_over
+
+        def transpose_e(t):
+            e_ps = psum.tile([P, E_PASSES * PAIR, P], F32, tag="e_t")
+            for j in range(E_PASSES * PAIR):
+                nc.tensor.transpose(
+                    out=e_ps[:, j, :], in_=e_rows[t][:].bitcast(F32)[:, j * P : (j + 1) * P], identity=ident_f32[:]
+                )
+            e_group = work.tile([P, E_PASSES * P * PACK], BF16, align_bytes=64)
+            nc.scalar.copy(
+                out=e_group[:].bitcast(F32).rearrange("p (g n u) -> p g n u", g=E_PASSES, u=PAIR),
+                in_=e_ps[:].rearrange("p (g u) n -> p g n u", u=PAIR),
+            )
+            e_grouped[t] = e_group
+
+        def quantise_e(t):
+            e_word = work.tile([P, E_PASSES * P], U32, align_bytes=64, bufs=4)
+            e_scale = work.tile([P, E_PASSES * P], U8, align_bytes=64, bufs=4)
+            nc.vector.quantize_mx(out=e_word[:].bitcast(FP8X4), scales=e_scale[:], in_=e_grouped[t][:])
+            e_words[t], e_plane[t] = e_word, e_scale
+
+        def attend(t):
+            b = t // TILES_PER_BATCH
+            grp, i = divmod(t, GROUP)
+            o_ps = psum.tile([P, DV], F32, tag="o_rows")
+            for g in range(E_PASSES):
+                nc.tensor.matmul_mx(
+                    out=o_ps[:],
+                    lhsT=e_words[t][:, g * P : (g + 1) * P].bitcast(FP8X4),
+                    lhsT_scale=e_plane[t][:, g * P : (g + 1) * P],
+                    rhs=v_words[b][:, g * DV : (g + 1) * DV].bitcast(FP8X4),
+                    rhs_scale=v_plane[b][:, g * DV : (g + 1) * DV],
+                    start=(g == 0),
+                    stop=(g == E_PASSES - 1),
+                )
+            o_tile = work.tile([P, DV], BF16)
+            nc.scalar.activation(out=o_tile[:], in_=o_ps[:], func=ACT.Copy, scale=recip[grp][:, i : i + 1])
+            o_rows[t] = o_tile
+
+        def transpose_o(t):
+            o_ps = psum.tile([P, PAIR, P], F32, tag="o_t")
+            for u in range(PAIR):
+                nc.tensor.transpose(
+                    out=o_ps[:, u, :], in_=o_rows[t][:].bitcast(F32)[:, u * P : (u + 1) * P], identity=ident_f32[:]
+                )
+            o_group = work.tile([P, P * PACK], BF16, align_bytes=64)
+            nc.vector.tensor_copy(
+                out=o_group[:].bitcast(F32).rearrange("p (n u) -> p n u", u=PAIR),
+                in_=o_ps[:].rearrange("p u n -> p n u"),
+            )
+            o_grouped[t] = o_group
+
+        def quantise_o(t):
+            grp, i = divmod(t, GROUP)
+            if i == 0:
+                o_words[grp] = work.tile([P, BANK], U32, name="o_word", align_bytes=64, bufs=2)
+                o_plane[grp] = work.tile([P, BANK], U8, name="o_scale", align_bytes=64, bufs=2)
+            nc.vector.quantize_mx(
+                out=o_words[grp][:, i * P : (i + 1) * P].bitcast(FP8X4),
+                scales=o_plane[grp][:, i * P : (i + 1) * P],
+                in_=o_grouped[t][:],
+            )
+
+        def project(grp):
+            b, first = divmod(grp * GROUP, TILES_PER_BATCH)
+            cols = slice(first * P, first * P + BANK)
+            y_ps = psum.tile([P, BANK], F32, tag="misc")
+            nc.tensor.matmul_mx(
+                out=y_ps[:],
+                lhsT=wo_words[:].bitcast(FP8X4),
+                lhsT_scale=wo_plane[:],
+                rhs=o_words[grp][:].bitcast(FP8X4),
+                rhs_scale=o_plane[grp][:],
+                start=True,
+                stop=True,
+            )
+            result = work.tile([P, BANK], F32)
+            nc.vector.scalar_tensor_tensor(
+                out=result[:], in0=y_ps[:], scalar=gamma_f32[:, 0:1], in1=x_sb[b][:, cols], op0=ALU.mult, op1=ALU.add
+            )
+            nc.sync.dma_start(out=out_cols[b][:, cols], in_=result[:])
+
+        def is_tile(t):
+            return 0 <= t < TILES
+
+        def starts_group(t):
+            return t % GROUP == 0 and 0 <= t < TILES
+
+        for step in range(-3, TILES + 7):
+            if is_tile(step):
+                exponentials(step)
+            if starts_group(step - 4):
+                reciprocal_sums((step - 4) // GROUP)
+            if is_tile(step + 1):
+                half_maxima(step + 1)
+            if is_tile(step - 2):
+                quantise_e(step - 2)
+            if is_tile(step + 1):
+                negated_maximum(step + 1)
+
+            if step == -1:
+                widen_gamma()
+                quantise_wo()
+            if 0 <= step < V_CHUNKS:
+                transpose_v(0, step, nc.scalar.copy)
+            later_chunk, phase = divmod(step, V_LATER_EVERY)
+            prepares_later_chunk = phase == V_LATER_EVERY - 1 and 0 <= later_chunk < V_CHUNKS
+            if prepares_later_chunk:
+                transpose_v(1, later_chunk, nc.vector.tensor_copy)
+
+            if is_tile(step - 5):
+                transpose_o(step - 5)
+            if is_tile(step - 1):
+                transpose_e(step - 1)
+            if starts_group(step + 3):
+                transpose_q((step + 3) // GROUP)
+            if is_tile(step - 4):
+                attend(step - 4)
+            if starts_group(step - 10):
+                project((step - 10) // GROUP)
+            if is_tile(step + 2):
+                scores(step + 2)
+            if is_tile(step - 6):
+                quantise_o(step - 6)
+            if 0 <= step < V_CHUNKS:
+                quantise_v(0, step)
+            if prepares_later_chunk:
+                quantise_v(1, later_chunk)

@@ -25,11 +25,11 @@ E_PASSES = M // K_PASS
 TILES_PER_BATCH = N // P
 TILES = B * TILES_PER_BATCH
 GROUP = BANK // P
-GROUPS = TILES // GROUP
 Q_HEAD = 2 * GROUP
+SCORE_BANKS = 2 * HALVES
+ROW_BANKS = 2
 V_CHUNKS = 4
 V_CHUNK_COLS = E_PASSES * DV // V_CHUNKS
-V_LATER_EVERY = 8
 
 
 def tile_selfattention_pb_t_kernel(tc, q, k, v, Wo, gamma, x, out):
@@ -51,6 +51,7 @@ def tile_selfattention_pb_t_kernel(tc, q, k, v, Wo, gamma, x, out):
         x_sb = [keep.tile([P, N], BF16, name="x_sb%d" % b) for b in range(B)]
         wo_sb = keep.tile([P, DV], BF16)
         gamma_bf16 = keep.tile([P, 1], BF16)
+        gamma_f32 = keep.tile([P, 1], F32)
 
         q_rows = [q[b].rearrange("(t p) d -> p t d", p=P) for b in range(B)]
         v_rows = [v[b].rearrange("(j p) m -> p j m", p=P) for b in range(B)]
@@ -69,8 +70,6 @@ def tile_selfattention_pb_t_kernel(tc, q, k, v, Wo, gamma, x, out):
         nc.sync.dma_start(out=q_sb[1][:], in_=q_rows[1])
         nc.sync.dma_start(out=x_sb[1][:], in_=x_cols[1])
 
-        gamma_f32 = keep.tile([P, 1], F32)
-
         v_grouped = [
             keep.tile([P, E_PASSES * DV * PACK], BF16, name="v_grouped%d" % b, align_bytes=64)
             for b in range(B)
@@ -81,28 +80,32 @@ def tile_selfattention_pb_t_kernel(tc, q, k, v, Wo, gamma, x, out):
         wo_words = keep.tile([P, C], U32, align_bytes=64)
         wo_plane = keep.tile([P, C], U8, align_bytes=64)
 
-        q_cols, score_banks, half_maxima_of, neg_max, half_sums, recip = {}, {}, {}, {}, {}, {}
-        e_rows, e_grouped, e_words, e_plane = {}, {}, {}, {}
-        o_rows, o_grouped, o_words, o_plane = {}, {}, {}, {}
+        wo_bank, v_bank, q_bank, q_cols = {}, {}, {}, {}
+        score_banks, half_max, neg_max, half_sums, row_sums, recip = {}, {}, {}, {}, {}, {}
+        e_rows, e_bank, e_grouped, e_words, e_plane = {}, {}, {}, {}, {}
+        o_row_bank, o_rows, o_bank, o_grouped, o_words, o_plane, y_bank = {}, {}, {}, {}, {}, {}, {}
 
-        def quantise_wo():
-            wo_ps = psum.tile([P, PAIR, C], F32, tag="misc")
+        def transpose_wo():
+            wo_ps = psum.tile([P, PAIR, C], F32, tag="rows", bufs=ROW_BANKS)
             for u in range(PAIR):
                 nc.tensor.transpose(
                     out=wo_ps[:, u, :], in_=wo_sb[:].bitcast(F32)[:, u * P : (u + 1) * P], identity=ident_f32[:]
                 )
+            wo_bank[0] = wo_ps
+
+        def regroup_wo():
             nc.scalar.copy(
                 out=wo_grouped[:].bitcast(F32).rearrange("p (c u) -> p c u", u=PAIR),
-                in_=wo_ps[:].rearrange("p u c -> p c u"),
+                in_=wo_bank[0][:].rearrange("p u c -> p c u"),
             )
-            nc.vector.quantize_mx(out=wo_words[:].bitcast(FP8X4), scales=wo_plane[:], in_=wo_grouped[:])
 
-        def widen_gamma():
+        def quantise_wo_and_widen_gamma():
+            nc.vector.quantize_mx(out=wo_words[:].bitcast(FP8X4), scales=wo_plane[:], in_=wo_grouped[:])
             nc.vector.tensor_copy(out=gamma_f32[:], in_=gamma_bf16[:])
 
-        def transpose_v(b, chunk, copy_out):
+        def transpose_v(b, chunk, tag, bufs):
             g, h = divmod(chunk, PAIR)
-            v_ps = psum.tile([P, PAIR, PAIR, P], F32, tag="misc")
+            v_ps = psum.tile([P, PAIR, PAIR, P], F32, tag=tag, bufs=bufs)
             for j in range(PAIR):
                 for u in range(PAIR):
                     first_word = (PAIR * h + j) * (M // PAIR) + (PAIR * g + u) * P
@@ -111,11 +114,14 @@ def tile_selfattention_pb_t_kernel(tc, q, k, v, Wo, gamma, x, out):
                         in_=v_sb[b][:].bitcast(F32)[:, first_word : first_word + P],
                         identity=ident_f32[:],
                     )
+            v_bank[(b, chunk)] = v_ps
+
+        def regroup_v(b, chunk, copy_out):
             copy_out(
                 out=v_grouped[b][:]
                 .bitcast(F32)
                 .rearrange("p (ch j c u) -> p ch j c u", ch=V_CHUNKS, j=PAIR, u=PAIR)[:, chunk],
-                in_=v_ps[:].rearrange("p j u c -> p j c u"),
+                in_=v_bank[(b, chunk)][:].rearrange("p j u c -> p j c u"),
             )
 
         def quantise_v(b, chunk):
@@ -128,20 +134,23 @@ def tile_selfattention_pb_t_kernel(tc, q, k, v, Wo, gamma, x, out):
 
         def transpose_q(grp):
             b, first = divmod(grp * GROUP, TILES_PER_BATCH)
-            q_ps = psum.tile([P, GROUP * P], BF16, tag="misc")
+            q_ps = psum.tile([P, GROUP * P], BF16, tag="rows", bufs=ROW_BANKS)
             for i in range(GROUP):
                 nc.tensor.transpose(
                     out=q_ps[:, i * P : (i + 1) * P], in_=q_sb[b][:, first + i, :], identity=ident_bf16[:]
                 )
+            q_bank[grp] = q_ps
+
+        def copy_q(grp):
             q_t = work.tile([P, GROUP * P], BF16)
-            nc.vector.tensor_copy(out=q_t[:], in_=q_ps[:])
+            nc.vector.tensor_copy(out=q_t[:], in_=q_bank[grp][:])
             q_cols[grp] = q_t
 
         def scores(t):
             grp, i = divmod(t, GROUP)
             banks = []
             for h in range(HALVES):
-                bank = psum.tile([P, BANK], F32, tag="scores", bufs=2 * HALVES)
+                bank = psum.tile([P, BANK], F32, tag="scores", bufs=SCORE_BANKS)
                 nc.tensor.matmul(
                     out=bank[:],
                     lhsT=q_cols[grp][:, i * P : (i + 1) * P],
@@ -158,13 +167,11 @@ def tile_selfattention_pb_t_kernel(tc, q, k, v, Wo, gamma, x, out):
                 nc.vector.tensor_reduce(
                     out=maxima[:, h : h + 1], in_=score_banks[t][h][:], axis=ALONG_FREE, op=ALU.max
                 )
-            half_maxima_of[t] = maxima
+            half_max[t] = maxima
 
         def negated_maximum(t):
             minus_max = work.tile([P, 1], F32)
-            nc.vector.tensor_reduce(
-                out=minus_max[:], in_=half_maxima_of[t][:], axis=ALONG_FREE, op=ALU.max, negate=True
-            )
+            nc.vector.tensor_reduce(out=minus_max[:], in_=half_max[t][:], axis=ALONG_FREE, op=ALU.max, negate=True)
             neg_max[t] = minus_max
 
         def exponentials(t):
@@ -183,11 +190,14 @@ def tile_selfattention_pb_t_kernel(tc, q, k, v, Wo, gamma, x, out):
                 )
             e_rows[t] = e_tile
 
-        def reciprocal_sums(grp):
+        def add_half_sums(grp):
             row_sum = work.tile([P, GROUP], F32)
             nc.vector.tensor_reduce(out=row_sum[:], in_=half_sums[grp][:], axis=ALONG_FREE, op=ALU.add)
+            row_sums[grp] = row_sum
+
+        def reciprocal_sums(grp):
             one_over = work.tile([P, GROUP], F32)
-            nc.vector.reciprocal(out=one_over[:], in_=row_sum[:])
+            nc.vector.reciprocal(out=one_over[:], in_=row_sums[grp][:])
             recip[grp] = one_over
 
         def transpose_e(t):
@@ -196,10 +206,13 @@ def tile_selfattention_pb_t_kernel(tc, q, k, v, Wo, gamma, x, out):
                 nc.tensor.transpose(
                     out=e_ps[:, j, :], in_=e_rows[t][:].bitcast(F32)[:, j * P : (j + 1) * P], identity=ident_f32[:]
                 )
+            e_bank[t] = e_ps
+
+        def regroup_e(t):
             e_group = work.tile([P, E_PASSES * P * PACK], BF16, align_bytes=64)
             nc.scalar.copy(
                 out=e_group[:].bitcast(F32).rearrange("p (g n u) -> p g n u", g=E_PASSES, u=PAIR),
-                in_=e_ps[:].rearrange("p (g u) n -> p g n u", u=PAIR),
+                in_=e_bank[t][:].rearrange("p (g u) n -> p g n u", u=PAIR),
             )
             e_grouped[t] = e_group
 
@@ -211,8 +224,7 @@ def tile_selfattention_pb_t_kernel(tc, q, k, v, Wo, gamma, x, out):
 
         def attend(t):
             b = t // TILES_PER_BATCH
-            grp, i = divmod(t, GROUP)
-            o_ps = psum.tile([P, DV], F32, tag="o_rows")
+            o_ps = psum.tile([P, DV], F32, tag="rows", bufs=ROW_BANKS)
             for g in range(E_PASSES):
                 nc.tensor.matmul_mx(
                     out=o_ps[:],
@@ -223,8 +235,14 @@ def tile_selfattention_pb_t_kernel(tc, q, k, v, Wo, gamma, x, out):
                     start=(g == 0),
                     stop=(g == E_PASSES - 1),
                 )
+            o_row_bank[t] = o_ps
+
+        def divide_o(t):
+            grp, i = divmod(t, GROUP)
             o_tile = work.tile([P, DV], BF16)
-            nc.scalar.activation(out=o_tile[:], in_=o_ps[:], func=ACT.Copy, scale=recip[grp][:, i : i + 1])
+            nc.scalar.activation(
+                out=o_tile[:], in_=o_row_bank[t][:], func=ACT.Copy, scale=recip[grp][:, i : i + 1]
+            )
             o_rows[t] = o_tile
 
         def transpose_o(t):
@@ -233,10 +251,13 @@ def tile_selfattention_pb_t_kernel(tc, q, k, v, Wo, gamma, x, out):
                 nc.tensor.transpose(
                     out=o_ps[:, u, :], in_=o_rows[t][:].bitcast(F32)[:, u * P : (u + 1) * P], identity=ident_f32[:]
                 )
+            o_bank[t] = o_ps
+
+        def regroup_o(t):
             o_group = work.tile([P, P * PACK], BF16, align_bytes=64)
             nc.vector.tensor_copy(
                 out=o_group[:].bitcast(F32).rearrange("p (n u) -> p n u", u=PAIR),
-                in_=o_ps[:].rearrange("p u n -> p n u"),
+                in_=o_bank[t][:].rearrange("p u n -> p n u"),
             )
             o_grouped[t] = o_group
 
@@ -252,9 +273,7 @@ def tile_selfattention_pb_t_kernel(tc, q, k, v, Wo, gamma, x, out):
             )
 
         def project(grp):
-            b, first = divmod(grp * GROUP, TILES_PER_BATCH)
-            cols = slice(first * P, first * P + BANK)
-            y_ps = psum.tile([P, BANK], F32, tag="misc")
+            y_ps = psum.tile([P, BANK], F32, tag="rows", bufs=ROW_BANKS)
             nc.tensor.matmul_mx(
                 out=y_ps[:],
                 lhsT=wo_words[:].bitcast(FP8X4),
@@ -264,9 +283,19 @@ def tile_selfattention_pb_t_kernel(tc, q, k, v, Wo, gamma, x, out):
                 start=True,
                 stop=True,
             )
+            y_bank[grp] = y_ps
+
+        def finish(grp):
+            b, first = divmod(grp * GROUP, TILES_PER_BATCH)
+            cols = slice(first * P, first * P + BANK)
             result = work.tile([P, BANK], F32)
             nc.vector.scalar_tensor_tensor(
-                out=result[:], in0=y_ps[:], scalar=gamma_f32[:, 0:1], in1=x_sb[b][:, cols], op0=ALU.mult, op1=ALU.add
+                out=result[:],
+                in0=y_bank[grp][:],
+                scalar=gamma_f32[:, 0:1],
+                in1=x_sb[b][:, cols],
+                op0=ALU.mult,
+                op1=ALU.add,
             )
             nc.sync.dma_start(out=out_cols[b][:, cols], in_=result[:])
 
@@ -276,43 +305,63 @@ def tile_selfattention_pb_t_kernel(tc, q, k, v, Wo, gamma, x, out):
         def starts_group(t):
             return t % GROUP == 0 and 0 <= t < TILES
 
-        for step in range(-3, TILES + 7):
+        def is_chunk(c):
+            return 0 <= c < V_CHUNKS
+
+        for step in range(-7, TILES + 9):
+            if is_chunk(step - 1):
+                quantise_v(0, step - 1)
+            if is_tile(step - 4):
+                attend(step - 4)
             if is_tile(step):
                 exponentials(step)
-            if starts_group(step - 4):
-                reciprocal_sums((step - 4) // GROUP)
+            if is_tile(step - 1):
+                regroup_e(step - 1)
+            if step == -4:
+                regroup_wo()
+            if is_chunk(step):
+                regroup_v(0, step, nc.scalar.copy)
+            if is_tile(step - 4):
+                divide_o(step - 4)
+
             if is_tile(step + 1):
                 half_maxima(step + 1)
             if is_tile(step - 2):
                 quantise_e(step - 2)
             if is_tile(step + 1):
                 negated_maximum(step + 1)
+            if starts_group(step - 3):
+                add_half_sums((step - 3) // GROUP)
+            if is_tile(step - 6):
+                regroup_o(step - 6)
+            if is_tile(step - 7):
+                quantise_o(step - 7)
+            if starts_group(step + 6):
+                copy_q((step + 6) // GROUP)
+            if starts_group(step - 12):
+                finish((step - 12) // GROUP)
+            if is_chunk(step - 2):
+                regroup_v(1, step - 2, nc.vector.tensor_copy)
+            if is_chunk(step - 3):
+                quantise_v(1, step - 3)
+            if step == -3:
+                quantise_wo_and_widen_gamma()
+            if starts_group(step - 3):
+                reciprocal_sums((step - 3) // GROUP)
 
-            if step == -1:
-                widen_gamma()
-                quantise_wo()
-            if 0 <= step < V_CHUNKS:
-                transpose_v(0, step, nc.scalar.copy)
-            later_chunk, phase = divmod(step, V_LATER_EVERY)
-            prepares_later_chunk = phase == V_LATER_EVERY - 1 and 0 <= later_chunk < V_CHUNKS
-            if prepares_later_chunk:
-                transpose_v(1, later_chunk, nc.vector.tensor_copy)
-
-            if is_tile(step - 5):
-                transpose_o(step - 5)
-            if is_tile(step - 1):
-                transpose_e(step - 1)
-            if starts_group(step + 3):
-                transpose_q((step + 3) // GROUP)
-            if is_tile(step - 4):
-                attend(step - 4)
-            if starts_group(step - 10):
-                project((step - 10) // GROUP)
+            if starts_group(step - 11):
+                project((step - 11) // GROUP)
             if is_tile(step + 2):
                 scores(step + 2)
-            if is_tile(step - 6):
-                quantise_o(step - 6)
-            if 0 <= step < V_CHUNKS:
-                quantise_v(0, step)
-            if prepares_later_chunk:
-                quantise_v(1, later_chunk)
+            if starts_group(step + 7):
+                transpose_q((step + 7) // GROUP)
+            if is_tile(step):
+                transpose_e(step)
+            if is_tile(step - 5):
+                transpose_o(step - 5)
+            if step == -5:
+                transpose_wo()
+            if is_chunk(step + 1):
+                transpose_v(0, step + 1, "rows", ROW_BANKS)
+            if is_chunk(step - 1):
+                transpose_v(1, step - 1, "o_t", 1)

@@ -28,6 +28,7 @@ GROUP = BANK // P
 Q_HEAD = 2 * GROUP
 SCORE_BANKS = 2 * HALVES
 ROW_BANKS = 2
+VECTOR_TURN = 2
 V_CHUNKS = 4
 V_CHUNK_COLS = E_PASSES * DV // V_CHUNKS
 
@@ -58,8 +59,8 @@ def tile_selfattention_pb_t_kernel(tc, q, k, v, Wo, gamma, x, out):
         x_cols = [x[b].rearrange("c h w -> c (h w)") for b in range(B)]
         out_cols = [out[b].rearrange("c h w -> c (h w)") for b in range(B)]
 
-        nc.sync.dma_start(out=k_sb[0][:], in_=k[0])
         nc.sync.dma_start(out=q_sb[0][:, 0:Q_HEAD, :], in_=q_rows[0][:, 0:Q_HEAD, :])
+        nc.sync.dma_start(out=k_sb[0][:], in_=k[0])
         nc.sync.dma_start(out=wo_sb[:], in_=Wo)
         nc.sync.dma_start(out=gamma_bf16[:], in_=gamma.partition_broadcast(P))
         nc.sync.dma_start(out=v_sb[0][:].rearrange("p (j m) -> p j m", m=M), in_=v_rows[0])
@@ -171,7 +172,14 @@ def tile_selfattention_pb_t_kernel(tc, q, k, v, Wo, gamma, x, out):
 
         def negated_maximum(t):
             minus_max = work.tile([P, 1], F32)
-            nc.vector.tensor_reduce(out=minus_max[:], in_=half_max[t][:], axis=ALONG_FREE, op=ALU.max, negate=True)
+            nc.gpsimd.tensor_scalar(
+                out=minus_max[:],
+                in0=half_max[t][:, 0:1],
+                scalar1=half_max[t][:, 1:2],
+                scalar2=-1.0,
+                op0=ALU.max,
+                op1=ALU.mult,
+            )
             neg_max[t] = minus_max
 
         def exponentials(t):
@@ -192,7 +200,9 @@ def tile_selfattention_pb_t_kernel(tc, q, k, v, Wo, gamma, x, out):
 
         def add_half_sums(grp):
             row_sum = work.tile([P, GROUP], F32)
-            nc.vector.tensor_reduce(out=row_sum[:], in_=half_sums[grp][:], axis=ALONG_FREE, op=ALU.add)
+            nc.gpsimd.tensor_tensor(
+                out=row_sum[:], in0=half_sums[grp][:, :, 0], in1=half_sums[grp][:, :, 1], op=ALU.add
+            )
             row_sums[grp] = row_sum
 
         def reciprocal_sums(grp):
@@ -208,9 +218,9 @@ def tile_selfattention_pb_t_kernel(tc, q, k, v, Wo, gamma, x, out):
                 )
             e_bank[t] = e_ps
 
-        def regroup_e(t):
+        def regroup_e(t, copy_out):
             e_group = work.tile([P, E_PASSES * P * PACK], BF16, align_bytes=64)
-            nc.scalar.copy(
+            copy_out(
                 out=e_group[:].bitcast(F32).rearrange("p (g n u) -> p g n u", g=E_PASSES, u=PAIR),
                 in_=e_bank[t][:].rearrange("p (g u) n -> p g n u", u=PAIR),
             )
@@ -308,16 +318,21 @@ def tile_selfattention_pb_t_kernel(tc, q, k, v, Wo, gamma, x, out):
         def is_chunk(c):
             return 0 <= c < V_CHUNKS
 
+        def is_vectors_turn(t):
+            return t % GROUP == VECTOR_TURN
+
         for step in range(-7, TILES + 9):
+            if step == -1:
+                transpose_wo()
             if is_chunk(step - 1):
                 quantise_v(0, step - 1)
             if is_tile(step - 4):
                 attend(step - 4)
             if is_tile(step):
                 exponentials(step)
-            if is_tile(step - 1):
-                regroup_e(step - 1)
-            if step == -4:
+            if is_tile(step - 1) and not is_vectors_turn(step - 1):
+                regroup_e(step - 1, nc.scalar.copy)
+            if step == -1:
                 regroup_wo()
             if is_chunk(step):
                 regroup_v(0, step, nc.scalar.copy)
@@ -332,6 +347,8 @@ def tile_selfattention_pb_t_kernel(tc, q, k, v, Wo, gamma, x, out):
                 negated_maximum(step + 1)
             if starts_group(step - 3):
                 add_half_sums((step - 3) // GROUP)
+            if is_tile(step - 1) and is_vectors_turn(step - 1):
+                regroup_e(step - 1, nc.vector.tensor_copy)
             if is_tile(step - 6):
                 regroup_o(step - 6)
             if is_tile(step - 7):
@@ -344,7 +361,7 @@ def tile_selfattention_pb_t_kernel(tc, q, k, v, Wo, gamma, x, out):
                 regroup_v(1, step - 2, nc.vector.tensor_copy)
             if is_chunk(step - 3):
                 quantise_v(1, step - 3)
-            if step == -3:
+            if step == 0:
                 quantise_wo_and_widen_gamma()
             if starts_group(step - 3):
                 reciprocal_sums((step - 3) // GROUP)
@@ -359,8 +376,6 @@ def tile_selfattention_pb_t_kernel(tc, q, k, v, Wo, gamma, x, out):
                 transpose_e(step)
             if is_tile(step - 5):
                 transpose_o(step - 5)
-            if step == -5:
-                transpose_wo()
             if is_chunk(step + 1):
                 transpose_v(0, step + 1, "rows", ROW_BANKS)
             if is_chunk(step - 1):

@@ -29,6 +29,10 @@ Q_HEAD = 2 * GROUP
 SCORE_BANKS = 2 * HALVES
 ROW_BANKS = 2
 VECTOR_TURN = 2
+DRAIN = TILES - 3
+SWAP = TILES - 6
+RECIPROCALS = [(t, GROUP) for t in range(0, TILES - GROUP, GROUP)] + [(TILES - GROUP, GROUP - 1), (TILES - 1, 1)]
+OUTPUTS = [(t, GROUP) for t in range(0, TILES - GROUP, GROUP)] + [(TILES - 4, 2), (TILES - 2, 1), (TILES - 1, 1)]
 V_CHUNKS = 4
 V_CHUNK_COLS = E_PASSES * DV // V_CHUNKS
 
@@ -59,8 +63,9 @@ def tile_selfattention_pb_t_kernel(tc, q, k, v, Wo, gamma, x, out):
         x_cols = [x[b].rearrange("c h w -> c (h w)") for b in range(B)]
         out_cols = [out[b].rearrange("c h w -> c (h w)") for b in range(B)]
 
-        nc.sync.dma_start(out=q_sb[0][:, 0:Q_HEAD, :], in_=q_rows[0][:, 0:Q_HEAD, :])
+        nc.sync.dma_start(out=q_sb[0][:, 0:GROUP, :], in_=q_rows[0][:, 0:GROUP, :])
         nc.sync.dma_start(out=k_sb[0][:], in_=k[0])
+        nc.sync.dma_start(out=q_sb[0][:, GROUP:Q_HEAD, :], in_=q_rows[0][:, GROUP:Q_HEAD, :])
         nc.sync.dma_start(out=wo_sb[:], in_=Wo)
         nc.sync.dma_start(out=gamma_bf16[:], in_=gamma.partition_broadcast(P))
         nc.sync.dma_start(out=v_sb[0][:].rearrange("p (j m) -> p j m", m=M), in_=v_rows[0])
@@ -198,20 +203,28 @@ def tile_selfattention_pb_t_kernel(tc, q, k, v, Wo, gamma, x, out):
                 )
             e_rows[t] = e_tile
 
-        def add_half_sums(grp):
-            row_sum = work.tile([P, GROUP], F32)
+        def add_half_sums(first, count):
+            grp, i = divmod(first, GROUP)
+            row_sum = work.tile([P, count], F32, name="row_sum%d" % count)
             nc.gpsimd.tensor_tensor(
-                out=row_sum[:], in0=half_sums[grp][:, :, 0], in1=half_sums[grp][:, :, 1], op=ALU.add
+                out=row_sum[:],
+                in0=half_sums[grp][:, i : i + count, 0],
+                in1=half_sums[grp][:, i : i + count, 1],
+                op=ALU.add,
             )
-            row_sums[grp] = row_sum
+            row_sums[first] = row_sum
 
-        def reciprocal_sums(grp):
-            one_over = work.tile([P, GROUP], F32)
-            nc.vector.reciprocal(out=one_over[:], in_=row_sums[grp][:])
-            recip[grp] = one_over
+        def reciprocal_sums(first, count):
+            one_over = work.tile([P, count], F32, name="one_over%d" % count)
+            nc.vector.reciprocal(out=one_over[:], in_=row_sums[first][:])
+            for i in range(count):
+                recip[first + i] = one_over[:, i : i + 1]
 
         def transpose_e(t):
-            e_ps = psum.tile([P, E_PASSES * PAIR, P], F32, tag="e_t")
+            if t == TILES - 1:
+                e_ps = psum.tile([P, E_PASSES * PAIR, P], F32, tag="scores", bufs=SCORE_BANKS)
+            else:
+                e_ps = psum.tile([P, E_PASSES * PAIR, P], F32, tag="e_t")
             for j in range(E_PASSES * PAIR):
                 nc.tensor.transpose(
                     out=e_ps[:, j, :], in_=e_rows[t][:].bitcast(F32)[:, j * P : (j + 1) * P], identity=ident_f32[:]
@@ -247,25 +260,30 @@ def tile_selfattention_pb_t_kernel(tc, q, k, v, Wo, gamma, x, out):
                 )
             o_row_bank[t] = o_ps
 
-        def divide_o(t):
-            grp, i = divmod(t, GROUP)
+        def divide_o(t, on_vector):
             o_tile = work.tile([P, DV], BF16)
-            nc.scalar.activation(
-                out=o_tile[:], in_=o_row_bank[t][:], func=ACT.Copy, scale=recip[grp][:, i : i + 1]
-            )
+            if on_vector:
+                nc.vector.tensor_scalar(
+                    out=o_tile[:], in0=o_row_bank[t][:], scalar1=recip[t], scalar2=None, op0=ALU.mult
+                )
+            else:
+                nc.scalar.activation(out=o_tile[:], in_=o_row_bank[t][:], func=ACT.Copy, scale=recip[t])
             o_rows[t] = o_tile
 
         def transpose_o(t):
-            o_ps = psum.tile([P, PAIR, P], F32, tag="o_t")
+            if t >= TILES - 8 and t % 2:
+                o_ps = psum.tile([P, PAIR, P], F32, tag="scores", bufs=SCORE_BANKS)
+            else:
+                o_ps = psum.tile([P, PAIR, P], F32, tag="o_t")
             for u in range(PAIR):
                 nc.tensor.transpose(
                     out=o_ps[:, u, :], in_=o_rows[t][:].bitcast(F32)[:, u * P : (u + 1) * P], identity=ident_f32[:]
                 )
             o_bank[t] = o_ps
 
-        def regroup_o(t):
+        def regroup_o(t, copy_out):
             o_group = work.tile([P, P * PACK], BF16, align_bytes=64)
-            nc.vector.tensor_copy(
+            copy_out(
                 out=o_group[:].bitcast(F32).rearrange("p (n u) -> p n u", u=PAIR),
                 in_=o_bank[t][:].rearrange("p u n -> p n u"),
             )
@@ -282,26 +300,30 @@ def tile_selfattention_pb_t_kernel(tc, q, k, v, Wo, gamma, x, out):
                 in_=o_grouped[t][:],
             )
 
-        def project(grp):
-            y_ps = psum.tile([P, BANK], F32, tag="rows", bufs=ROW_BANKS)
+        def project(first, count):
+            grp, i = divmod(first, GROUP)
+            if first + count + 7 >= DRAIN:
+                y_ps = psum.tile([P, count * P], F32, tag="scores", bufs=SCORE_BANKS)
+            else:
+                y_ps = psum.tile([P, count * P], F32, tag="rows", bufs=ROW_BANKS)
             nc.tensor.matmul_mx(
                 out=y_ps[:],
                 lhsT=wo_words[:].bitcast(FP8X4),
                 lhsT_scale=wo_plane[:],
-                rhs=o_words[grp][:].bitcast(FP8X4),
-                rhs_scale=o_plane[grp][:],
+                rhs=o_words[grp][:, i * P : (i + count) * P].bitcast(FP8X4),
+                rhs_scale=o_plane[grp][:, i * P : (i + count) * P],
                 start=True,
                 stop=True,
             )
-            y_bank[grp] = y_ps
+            y_bank[first] = y_ps
 
-        def finish(grp):
-            b, first = divmod(grp * GROUP, TILES_PER_BATCH)
-            cols = slice(first * P, first * P + BANK)
-            result = work.tile([P, BANK], F32)
+        def finish(first, count):
+            b, i = divmod(first, TILES_PER_BATCH)
+            cols = slice(i * P, (i + count) * P)
+            result = work.tile([P, count * P], F32, name="result%d" % count)
             nc.vector.scalar_tensor_tensor(
                 out=result[:],
-                in0=y_bank[grp][:],
+                in0=y_bank[first][:],
                 scalar=gamma_f32[:, 0:1],
                 in1=x_sb[b][:, cols],
                 op0=ALU.mult,
@@ -318,65 +340,77 @@ def tile_selfattention_pb_t_kernel(tc, q, k, v, Wo, gamma, x, out):
         def is_chunk(c):
             return 0 <= c < V_CHUNKS
 
-        def is_vectors_turn(t):
-            return t % GROUP == VECTOR_TURN
+        def regroup_e_on_vector(t):
+            return t == 0 or t % GROUP == VECTOR_TURN and GROUP < t < DRAIN
 
         for step in range(-7, TILES + 9):
+            draining = step >= DRAIN
             if step == -1:
                 transpose_wo()
             if is_chunk(step - 1):
                 quantise_v(0, step - 1)
-            if is_tile(step - 4):
-                attend(step - 4)
+            for t in range(step - 4 + (step > DRAIN), step - 3 + draining):
+                if is_tile(t):
+                    attend(t)
             if is_tile(step):
                 exponentials(step)
-            if is_tile(step - 1) and not is_vectors_turn(step - 1):
+            if is_tile(step - 1) and not regroup_e_on_vector(step - 1):
                 regroup_e(step - 1, nc.scalar.copy)
             if step == -1:
                 regroup_wo()
-            if is_chunk(step):
-                regroup_v(0, step, nc.scalar.copy)
-            if is_tile(step - 4):
-                divide_o(step - 4)
+            if is_chunk(step - 0):
+                regroup_v(0, step - 0, nc.scalar.copy)
+            if is_tile(step - 4) and step - 4 < SWAP:
+                divide_o(step - 4, False)
+            if is_tile(step - 6) and step - 6 >= SWAP:
+                regroup_o(step - 6, nc.scalar.copy)
 
+            if is_tile(step - 4) and step - 4 >= SWAP:
+                divide_o(step - 4, True)
             if is_tile(step + 1):
                 half_maxima(step + 1)
             if is_tile(step - 2):
                 quantise_e(step - 2)
             if is_tile(step + 1):
                 negated_maximum(step + 1)
-            if starts_group(step - 3):
-                add_half_sums((step - 3) // GROUP)
-            if is_tile(step - 1) and is_vectors_turn(step - 1):
+            for first, count in RECIPROCALS:
+                if step == first + count - 1:
+                    add_half_sums(first, count)
+            if is_tile(step - 1) and regroup_e_on_vector(step - 1):
                 regroup_e(step - 1, nc.vector.tensor_copy)
-            if is_tile(step - 6):
-                regroup_o(step - 6)
+            if is_tile(step - 6) and step - 6 < SWAP:
+                regroup_o(step - 6, nc.vector.tensor_copy)
             if is_tile(step - 7):
                 quantise_o(step - 7)
-            if starts_group(step + 6):
-                copy_q((step + 6) // GROUP)
-            if starts_group(step - 12):
-                finish((step - 12) // GROUP)
+            for grp in range(TILES // GROUP):
+                if step == grp * GROUP - (5 if grp == 1 else 6):
+                    copy_q(grp)
+            for first, count in OUTPUTS:
+                if step == first + count + 8:
+                    finish(first, count)
             if is_chunk(step - 2):
                 regroup_v(1, step - 2, nc.vector.tensor_copy)
             if is_chunk(step - 3):
                 quantise_v(1, step - 3)
             if step == 0:
                 quantise_wo_and_widen_gamma()
-            if starts_group(step - 3):
-                reciprocal_sums((step - 3) // GROUP)
+            for first, count in RECIPROCALS:
+                if step == first + count - 1:
+                    reciprocal_sums(first, count)
 
-            if starts_group(step - 11):
-                project((step - 11) // GROUP)
+            for first, count in OUTPUTS:
+                if step == first + count + 7:
+                    project(first, count)
             if is_tile(step + 2):
                 scores(step + 2)
-            if starts_group(step + 7):
-                transpose_q((step + 7) // GROUP)
+            for grp in range(TILES // GROUP):
+                if step == grp * GROUP - (6 if grp == 1 else 7):
+                    transpose_q(grp)
             if is_tile(step):
                 transpose_e(step)
             if is_tile(step - 5):
                 transpose_o(step - 5)
-            if is_chunk(step + 1):
-                transpose_v(0, step + 1, "rows", ROW_BANKS)
+            if is_chunk(step - -1):
+                transpose_v(0, step - -1, "rows", ROW_BANKS)
             if is_chunk(step - 1):
                 transpose_v(1, step - 1, "o_t", 1)

@@ -28,6 +28,7 @@ GROUP = BANK // P
 Q_HEAD = 2 * GROUP
 SCORE_BANKS = 2 * HALVES
 ROW_BANKS = 2
+VECTOR_EVERY = 8
 VECTOR_TURN = 2
 DRAIN = TILES - 3
 SWAP = TILES - 6
@@ -341,7 +342,7 @@ def tile_selfattention_pb_t_kernel(tc, q, k, v, Wo, gamma, x, out):
             return 0 <= c < V_CHUNKS
 
         def regroup_e_on_vector(t):
-            return t == 0 or t % GROUP == VECTOR_TURN and GROUP < t < DRAIN
+            return t == 0 or t % VECTOR_EVERY == VECTOR_TURN and GROUP < t < DRAIN
 
         for step in range(-7, TILES + 9):
             draining = step >= DRAIN
@@ -360,26 +361,25 @@ def tile_selfattention_pb_t_kernel(tc, q, k, v, Wo, gamma, x, out):
                 regroup_wo()
             if is_chunk(step - 0):
                 regroup_v(0, step - 0, nc.scalar.copy)
-            if is_tile(step - 4) and step - 4 < SWAP:
-                divide_o(step - 4, False)
-            if is_tile(step - 6) and step - 6 >= SWAP:
-                regroup_o(step - 6, nc.scalar.copy)
 
             if is_tile(step - 4) and step - 4 >= SWAP:
                 divide_o(step - 4, True)
+            for first, count in RECIPROCALS:
+                if step == first + count:
+                    add_half_sums(first, count)
             if is_tile(step + 1):
                 half_maxima(step + 1)
+            for first, count in RECIPROCALS:
+                if step == first + count:
+                    reciprocal_sums(first, count)
+            if is_tile(step - 6) and step - 6 < SWAP:
+                regroup_o(step - 6, nc.vector.tensor_copy)
             if is_tile(step - 2):
                 quantise_e(step - 2)
             if is_tile(step + 1):
                 negated_maximum(step + 1)
-            for first, count in RECIPROCALS:
-                if step == first + count - 1:
-                    add_half_sums(first, count)
             if is_tile(step - 1) and regroup_e_on_vector(step - 1):
                 regroup_e(step - 1, nc.vector.tensor_copy)
-            if is_tile(step - 6) and step - 6 < SWAP:
-                regroup_o(step - 6, nc.vector.tensor_copy)
             if is_tile(step - 7):
                 quantise_o(step - 7)
             for grp in range(TILES // GROUP):
@@ -394,10 +394,11 @@ def tile_selfattention_pb_t_kernel(tc, q, k, v, Wo, gamma, x, out):
                 quantise_v(1, step - 3)
             if step == 0:
                 quantise_wo_and_widen_gamma()
-            for first, count in RECIPROCALS:
-                if step == first + count - 1:
-                    reciprocal_sums(first, count)
 
+            if is_tile(step - 4) and step - 4 < SWAP:
+                divide_o(step - 4, False)
+            if is_tile(step - 6) and step - 6 >= SWAP:
+                regroup_o(step - 6, nc.scalar.copy)
             for first, count in OUTPUTS:
                 if step == first + count + 7:
                     project(first, count)
@@ -406,10 +407,10 @@ def tile_selfattention_pb_t_kernel(tc, q, k, v, Wo, gamma, x, out):
             for grp in range(TILES // GROUP):
                 if step == grp * GROUP - (6 if grp == 1 else 7):
                     transpose_q(grp)
-            if is_tile(step):
-                transpose_e(step)
             if is_tile(step - 5):
                 transpose_o(step - 5)
+            if is_tile(step):
+                transpose_e(step)
             if is_chunk(step - -1):
                 transpose_v(0, step - -1, "rows", ROW_BANKS)
             if is_chunk(step - 1):

@@ -64,17 +64,27 @@ def tile_selfattention_pb_t_kernel(tc, q, k, v, Wo, gamma, x, out):
         x_cols = [x[b].rearrange("c h w -> c (h w)") for b in range(B)]
         out_cols = [out[b].rearrange("c h w -> c (h w)") for b in range(B)]
 
-        nc.sync.dma_start(out=q_sb[0][:, 0:GROUP, :], in_=q_rows[0][:, 0:GROUP, :])
+        def load_q(b, first, last):
+            nc.sync.dma_start(out=q_sb[b][:, first:last, :], in_=q_rows[b][:, first:last, :])
+
+        def load_v(b, first, last):
+            nc.sync.dma_start(
+                out=v_sb[b][:].rearrange("p (j m) -> p j m", m=M)[:, first:last, :], in_=v_rows[b][:, first:last, :]
+            )
+
+        load_q(0, 0, GROUP)
         nc.sync.dma_start(out=k_sb[0][:], in_=k[0])
-        nc.sync.dma_start(out=q_sb[0][:, GROUP:Q_HEAD, :], in_=q_rows[0][:, GROUP:Q_HEAD, :])
+        load_v(0, 0, 2)
         nc.sync.dma_start(out=wo_sb[:], in_=Wo)
         nc.sync.dma_start(out=gamma_bf16[:], in_=gamma.partition_broadcast(P))
-        nc.sync.dma_start(out=v_sb[0][:].rearrange("p (j m) -> p j m", m=M), in_=v_rows[0])
-        nc.sync.dma_start(out=q_sb[0][:, Q_HEAD:, :], in_=q_rows[0][:, Q_HEAD:, :])
-        nc.sync.dma_start(out=v_sb[1][:].rearrange("p (j m) -> p j m", m=M), in_=v_rows[1])
+        load_q(0, GROUP, 2 * GROUP)
+        load_v(0, 2, 4)
+        load_q(0, 2 * GROUP, 4 * GROUP)
+        load_v(1, 0, 4)
+        load_q(0, 4 * GROUP, TILES_PER_BATCH)
         nc.sync.dma_start(out=x_sb[0][:], in_=x_cols[0])
         nc.sync.dma_start(out=k_sb[1][:], in_=k[1])
-        nc.sync.dma_start(out=q_sb[1][:], in_=q_rows[1])
+        load_q(1, 0, TILES_PER_BATCH)
         nc.sync.dma_start(out=x_sb[1][:], in_=x_cols[1])
 
         v_grouped = [
@@ -139,19 +149,19 @@ def tile_selfattention_pb_t_kernel(tc, q, k, v, Wo, gamma, x, out):
                 in_=v_grouped[b][:, chunk * V_CHUNK_COLS * PACK : (chunk + 1) * V_CHUNK_COLS * PACK],
             )
 
-        def transpose_q(grp):
-            b, first = divmod(grp * GROUP, TILES_PER_BATCH)
-            q_ps = psum.tile([P, GROUP * P], BF16, tag="rows", bufs=ROW_BANKS)
-            for i in range(GROUP):
+        def transpose_q(grp, i=0, count=GROUP, tag="rows", bufs=ROW_BANKS):
+            b, first = divmod(grp * GROUP + i, TILES_PER_BATCH)
+            q_ps = psum.tile([P, count * P], BF16, tag=tag, bufs=bufs)
+            for j in range(count):
                 nc.tensor.transpose(
-                    out=q_ps[:, i * P : (i + 1) * P], in_=q_sb[b][:, first + i, :], identity=ident_bf16[:]
+                    out=q_ps[:, j * P : (j + 1) * P], in_=q_sb[b][:, first + j, :], identity=ident_bf16[:]
                 )
-            q_bank[grp] = q_ps
+            q_bank[(grp, i)] = q_ps
 
-        def copy_q(grp):
-            q_t = work.tile([P, GROUP * P], BF16)
-            nc.vector.tensor_copy(out=q_t[:], in_=q_bank[grp][:])
-            q_cols[grp] = q_t
+        def copy_q(grp, i=0, count=GROUP):
+            if i == 0:
+                q_cols[grp] = work.tile([P, GROUP * P], BF16, name="q_t")
+            nc.vector.tensor_copy(out=q_cols[grp][:, i * P : (i + count) * P], in_=q_bank[(grp, i)][:])
 
         def scores(t):
             grp, i = divmod(t, GROUP)
@@ -342,14 +352,35 @@ def tile_selfattention_pb_t_kernel(tc, q, k, v, Wo, gamma, x, out):
             return 0 <= c < V_CHUNKS
 
         def regroup_e_on_vector(t):
-            return t == 0 or t % VECTOR_EVERY == VECTOR_TURN and GROUP < t < DRAIN
+            return t % VECTOR_EVERY == VECTOR_TURN and GROUP < t < DRAIN
 
-        for step in range(-7, TILES + 9):
+        transpose_q(0, 0, 1, "e_t", 1)
+        copy_q(0, 0, 1)
+        transpose_q(0, 1, GROUP - 1)
+        copy_q(0, 1, GROUP - 1)
+        scores(0)
+        half_maxima(0)
+        negated_maximum(0)
+        scores(1)
+        half_maxima(1)
+        negated_maximum(1)
+        transpose_v(0, 0, "o_t", 1)
+        regroup_v(0, 0, nc.scalar.copy)
+        exponentials(0)
+        transpose_v(0, 2, "e_t", 1)
+        regroup_v(0, 2, nc.vector.tensor_copy)
+        transpose_v(0, 1, "o_t", 1)
+        transpose_v(0, 3, "rows", ROW_BANKS)
+        quantise_v(0, 0)
+        scores(2)
+        transpose_e(0)
+        transpose_q(1)
+        quantise_v(0, 2)
+
+        for step in range(1, TILES + 9):
             draining = step >= DRAIN
-            if step == -1:
+            if step == 4:
                 transpose_wo()
-            if is_chunk(step - 1):
-                quantise_v(0, step - 1)
             for t in range(step - 4 + (step > DRAIN), step - 3 + draining):
                 if is_tile(t):
                     attend(t)
@@ -357,10 +388,10 @@ def tile_selfattention_pb_t_kernel(tc, q, k, v, Wo, gamma, x, out):
                 exponentials(step)
             if is_tile(step - 1) and not regroup_e_on_vector(step - 1):
                 regroup_e(step - 1, nc.scalar.copy)
-            if step == -1:
+            if step == 4:
                 regroup_wo()
-            if is_chunk(step - 0):
-                regroup_v(0, step - 0, nc.scalar.copy)
+            if step == 1:
+                regroup_v(0, 1, nc.scalar.copy)
 
             if is_tile(step - 4) and step - 4 >= SWAP:
                 divide_o(step - 4, True)
@@ -374,8 +405,16 @@ def tile_selfattention_pb_t_kernel(tc, q, k, v, Wo, gamma, x, out):
                     reciprocal_sums(first, count)
             if is_tile(step - 6) and step - 6 < SWAP:
                 regroup_o(step - 6, nc.vector.tensor_copy)
+            if step == 1:
+                copy_q(1)
             if is_tile(step - 2):
                 quantise_e(step - 2)
+            if step == 1:
+                regroup_v(0, 3, nc.vector.tensor_copy)
+            if step == 2:
+                quantise_v(0, 1)
+            if step == 3:
+                quantise_v(0, 3)
             if is_tile(step + 1):
                 negated_maximum(step + 1)
             if is_tile(step - 1) and regroup_e_on_vector(step - 1):
@@ -383,7 +422,7 @@ def tile_selfattention_pb_t_kernel(tc, q, k, v, Wo, gamma, x, out):
             if is_tile(step - 7):
                 quantise_o(step - 7)
             for grp in range(TILES // GROUP):
-                if step == grp * GROUP - (5 if grp == 1 else 6):
+                if step == grp * GROUP - 6:
                     copy_q(grp)
             for first, count in OUTPUTS:
                 if step == first + count + 8:
@@ -392,7 +431,7 @@ def tile_selfattention_pb_t_kernel(tc, q, k, v, Wo, gamma, x, out):
                 regroup_v(1, step - 2, nc.vector.tensor_copy)
             if is_chunk(step - 3):
                 quantise_v(1, step - 3)
-            if step == 0:
+            if step == 5:
                 quantise_wo_and_widen_gamma()
 
             if is_tile(step - 4) and step - 4 < SWAP:
@@ -405,13 +444,11 @@ def tile_selfattention_pb_t_kernel(tc, q, k, v, Wo, gamma, x, out):
             if is_tile(step + 2):
                 scores(step + 2)
             for grp in range(TILES // GROUP):
-                if step == grp * GROUP - (6 if grp == 1 else 7):
+                if step == grp * GROUP - 7:
                     transpose_q(grp)
             if is_tile(step - 5):
                 transpose_o(step - 5)
             if is_tile(step):
                 transpose_e(step)
-            if is_chunk(step - -1):
-                transpose_v(0, step - -1, "rows", ROW_BANKS)
             if is_chunk(step - 1):
                 transpose_v(1, step - 1, "o_t", 1)

@@ -30,8 +30,10 @@ SCORE_BANKS = 2 * HALVES
 ROW_BANKS = 2
 VECTOR_EVERY = 8
 VECTOR_TURN = 2
+LAST = TILES - 1
 DRAIN = TILES - 3
-SWAP = TILES - 6
+V_DIVIDES = (TILES - 5, TILES - 4)
+S_REGROUPS = (TILES - 6, TILES - 4, TILES - 2)
 RECIPROCALS = [(t, GROUP) for t in range(0, TILES - GROUP, GROUP)] + [(TILES - GROUP, GROUP - 1), (TILES - 1, 1)]
 OUTPUTS = [(t, GROUP) for t in range(0, TILES - GROUP, GROUP)] + [(TILES - 4, 2), (TILES - 2, 1), (TILES - 1, 1)]
 V_CHUNKS = 4
@@ -72,8 +74,10 @@ def tile_selfattention_pb_t_kernel(tc, q, k, v, Wo, gamma, x, out):
                 out=v_sb[b][:].rearrange("p (j m) -> p j m", m=M)[:, first:last, :], in_=v_rows[b][:, first:last, :]
             )
 
-        load_q(0, 0, GROUP)
-        nc.sync.dma_start(out=k_sb[0][:], in_=k[0])
+        load_q(0, 0, 1)
+        nc.sync.dma_start(out=k_sb[0][:, 0:512], in_=k[0][:, 0:512])
+        load_q(0, 1, GROUP)
+        nc.sync.dma_start(out=k_sb[0][:, 512:1024], in_=k[0][:, 512:1024])
         load_v(0, 0, 2)
         nc.sync.dma_start(out=wo_sb[:], in_=Wo)
         nc.sync.dma_start(out=gamma_bf16[:], in_=gamma.partition_broadcast(P))
@@ -232,21 +236,20 @@ def tile_selfattention_pb_t_kernel(tc, q, k, v, Wo, gamma, x, out):
                 recip[first + i] = one_over[:, i : i + 1]
 
         def transpose_e(t):
-            if t == TILES - 1:
-                e_ps = psum.tile([P, E_PASSES * PAIR, P], F32, tag="scores", bufs=SCORE_BANKS)
-            else:
-                e_ps = psum.tile([P, E_PASSES * PAIR, P], F32, tag="e_t")
-            for j in range(E_PASSES * PAIR):
-                nc.tensor.transpose(
-                    out=e_ps[:, j, :], in_=e_rows[t][:].bitcast(F32)[:, j * P : (j + 1) * P], identity=ident_f32[:]
-                )
+            e_ps = psum.tile([P, E_PASSES, PAIR, P], F32, tag="e_t")
+            for g in range(E_PASSES):
+                for u in range(PAIR):
+                    first = (PAIR * g + u) * P
+                    nc.tensor.transpose(
+                        out=e_ps[:, g, u, :], in_=e_rows[t][:].bitcast(F32)[:, first : first + P], identity=ident_f32[:]
+                    )
             e_bank[t] = e_ps
 
         def regroup_e(t, copy_out):
             e_group = work.tile([P, E_PASSES * P * PACK], BF16, align_bytes=64)
             copy_out(
                 out=e_group[:].bitcast(F32).rearrange("p (g n u) -> p g n u", g=E_PASSES, u=PAIR),
-                in_=e_bank[t][:].rearrange("p (g u) n -> p g n u", u=PAIR),
+                in_=e_bank[t][:].rearrange("p g u n -> p g n u"),
             )
             e_grouped[t] = e_group
 
@@ -255,6 +258,32 @@ def tile_selfattention_pb_t_kernel(tc, q, k, v, Wo, gamma, x, out):
             e_scale = work.tile([P, E_PASSES * P], U8, align_bytes=64, bufs=4)
             nc.vector.quantize_mx(out=e_word[:].bitcast(FP8X4), scales=e_scale[:], in_=e_grouped[t][:])
             e_words[t], e_plane[t] = e_word, e_scale
+
+        def transpose_last_e(g):
+            e_ps = psum.tile([P, PAIR, P], F32, tag="scores", bufs=SCORE_BANKS)
+            for u in range(PAIR):
+                first = (PAIR * g + u) * P
+                nc.tensor.transpose(
+                    out=e_ps[:, u, :], in_=e_rows[LAST][:].bitcast(F32)[:, first : first + P], identity=ident_f32[:]
+                )
+            e_bank[(LAST, g)] = e_ps
+
+        def regroup_last_e(g, copy_out):
+            e_group = work.tile([P, P * PACK], BF16, name="last_e_group", align_bytes=64)
+            copy_out(
+                out=e_group[:].bitcast(F32).rearrange("p (n u) -> p n u", u=PAIR),
+                in_=e_bank[(LAST, g)][:].rearrange("p u n -> p n u"),
+            )
+            e_grouped[(LAST, g)] = e_group
+
+        def quantise_last_e(g):
+            if g == 0:
+                e_words[LAST] = work.tile([P, E_PASSES * P], U32, name="e_word", align_bytes=64, bufs=4)
+                e_plane[LAST] = work.tile([P, E_PASSES * P], U8, name="e_scale", align_bytes=64, bufs=4)
+            cols = slice(g * P, (g + 1) * P)
+            nc.vector.quantize_mx(
+                out=e_words[LAST][:, cols].bitcast(FP8X4), scales=e_plane[LAST][:, cols], in_=e_grouped[(LAST, g)][:]
+            )
 
         def attend(t):
             b = t // TILES_PER_BATCH
@@ -386,15 +415,19 @@ def tile_selfattention_pb_t_kernel(tc, q, k, v, Wo, gamma, x, out):
                     attend(t)
             if is_tile(step):
                 exponentials(step)
-            if is_tile(step - 1) and not regroup_e_on_vector(step - 1):
+            if is_tile(step - 1) and step - 1 < LAST and not regroup_e_on_vector(step - 1):
                 regroup_e(step - 1, nc.scalar.copy)
+            if step == LAST + 1:
+                regroup_last_e(1, nc.scalar.copy)
             if step == 4:
                 regroup_wo()
             if step == 1:
                 regroup_v(0, 1, nc.scalar.copy)
 
-            if is_tile(step - 4) and step - 4 >= SWAP:
+            if is_tile(step - 4) and step - 4 in V_DIVIDES:
                 divide_o(step - 4, True)
+            if step == LAST + 1:
+                regroup_last_e(0, nc.vector.tensor_copy)
             for first, count in RECIPROCALS:
                 if step == first + count:
                     add_half_sums(first, count)
@@ -403,12 +436,15 @@ def tile_selfattention_pb_t_kernel(tc, q, k, v, Wo, gamma, x, out):
             for first, count in RECIPROCALS:
                 if step == first + count:
                     reciprocal_sums(first, count)
-            if is_tile(step - 6) and step - 6 < SWAP:
+            if is_tile(step - 6) and step - 6 not in S_REGROUPS:
                 regroup_o(step - 6, nc.vector.tensor_copy)
             if step == 1:
                 copy_q(1)
-            if is_tile(step - 2):
+            if is_tile(step - 2) and step - 2 < LAST:
                 quantise_e(step - 2)
+            if step == LAST + 1:
+                quantise_last_e(0)
+                quantise_last_e(1)
             if step == 1:
                 regroup_v(0, 3, nc.vector.tensor_copy)
             if step == 2:
@@ -434,9 +470,9 @@ def tile_selfattention_pb_t_kernel(tc, q, k, v, Wo, gamma, x, out):
             if step == 5:
                 quantise_wo_and_widen_gamma()
 
-            if is_tile(step - 4) and step - 4 < SWAP:
+            if is_tile(step - 4) and step - 4 not in V_DIVIDES:
                 divide_o(step - 4, False)
-            if is_tile(step - 6) and step - 6 >= SWAP:
+            if is_tile(step - 6) and step - 6 in S_REGROUPS:
                 regroup_o(step - 6, nc.scalar.copy)
             for first, count in OUTPUTS:
                 if step == first + count + 7:
@@ -448,7 +484,10 @@ def tile_selfattention_pb_t_kernel(tc, q, k, v, Wo, gamma, x, out):
                     transpose_q(grp)
             if is_tile(step - 5):
                 transpose_o(step - 5)
-            if is_tile(step):
+            if is_tile(step) and step < LAST:
                 transpose_e(step)
+            if step == LAST:
+                for g in range(E_PASSES):
+                    transpose_last_e(g)
             if is_chunk(step - 1):
                 transpose_v(1, step - 1, "o_t", 1)

@@ -25,17 +25,17 @@ E_PASSES = M // K_PASS
 TILES_PER_BATCH = N // P
 TILES = B * TILES_PER_BATCH
 GROUP = BANK // P
-Q_HEAD = 2 * GROUP
 SCORE_BANKS = 2 * HALVES
 ROW_BANKS = 2
-VECTOR_EVERY = 8
-VECTOR_TURN = 2
 LAST = TILES - 1
+V_DIVIDES = (TILES - 6, TILES - 5)
+S_REGROUPS = TILES - 8
 DRAIN = TILES - 3
-V_DIVIDES = (TILES - 5, TILES - 4)
-S_REGROUPS = (TILES - 6, TILES - 4, TILES - 2)
+MIXED = 13
+SPREAD = 8
 RECIPROCALS = [(t, GROUP) for t in range(0, TILES - GROUP, GROUP)] + [(TILES - GROUP, GROUP - 1), (TILES - 1, 1)]
 OUTPUTS = [(t, GROUP) for t in range(0, TILES - GROUP, GROUP)] + [(TILES - 4, 2), (TILES - 2, 1), (TILES - 1, 1)]
+OUT_LATE = {MIXED - 2: 1, MIXED - 1: 3}
 V_CHUNKS = 4
 V_CHUNK_COLS = E_PASSES * DV // V_CHUNKS
 
@@ -74,10 +74,8 @@ def tile_selfattention_pb_t_kernel(tc, q, k, v, Wo, gamma, x, out):
                 out=v_sb[b][:].rearrange("p (j m) -> p j m", m=M)[:, first:last, :], in_=v_rows[b][:, first:last, :]
             )
 
-        load_q(0, 0, 1)
-        nc.sync.dma_start(out=k_sb[0][:, 0:512], in_=k[0][:, 0:512])
-        load_q(0, 1, GROUP)
-        nc.sync.dma_start(out=k_sb[0][:, 512:1024], in_=k[0][:, 512:1024])
+        load_q(0, 0, GROUP)
+        nc.sync.dma_start(out=k_sb[0][:], in_=k[0])
         load_v(0, 0, 2)
         nc.sync.dma_start(out=wo_sb[:], in_=Wo)
         nc.sync.dma_start(out=gamma_bf16[:], in_=gamma.partition_broadcast(P))
@@ -97,28 +95,51 @@ def tile_selfattention_pb_t_kernel(tc, q, k, v, Wo, gamma, x, out):
         ]
         v_words = [keep.tile([P, E_PASSES * DV], U32, name="v_words%d" % b, align_bytes=64) for b in range(B)]
         v_plane = [keep.tile([P, E_PASSES * DV], U8, name="v_plane%d" % b, align_bytes=64) for b in range(B)]
-        wo_grouped = keep.tile([P, C * PACK], BF16, align_bytes=64)
-        wo_words = keep.tile([P, C], U32, align_bytes=64)
-        wo_plane = keep.tile([P, C], U8, align_bytes=64)
+        wo_grouped = keep.tile([P, PAIR * C * PACK], BF16, align_bytes=64)
+        wo_words = keep.tile([P, PAIR * C], U32, align_bytes=64)
+        wo_plane = keep.tile([P, PAIR * C], U8, align_bytes=64)
+        recip_cols = [keep.tile([P, SPREAD], F32, name="recip_cols%d" % i) for i in range(4)]
+        for i in range(4):
+            nc.gpsimd.memset(recip_cols[i][:], 0.0)
 
         wo_bank, v_bank, q_bank, q_cols = {}, {}, {}, {}
         score_banks, half_max, neg_max, half_sums, row_sums, recip = {}, {}, {}, {}, {}, {}
         e_rows, e_bank, e_grouped, e_words, e_plane = {}, {}, {}, {}, {}
+        recip_rows, o_spread_bank, o_spread = {}, {}, {}
         o_row_bank, o_rows, o_bank, o_grouped, o_words, o_plane, y_bank = {}, {}, {}, {}, {}, {}, {}
 
-        def transpose_wo():
-            wo_ps = psum.tile([P, PAIR, C], F32, tag="rows", bufs=ROW_BANKS)
-            for u in range(PAIR):
-                nc.tensor.transpose(
-                    out=wo_ps[:, u, :], in_=wo_sb[:].bitcast(F32)[:, u * P : (u + 1) * P], identity=ident_f32[:]
-                )
-            wo_bank[0] = wo_ps
+        def is_spread(t):
+            return t in range(1, MIXED * GROUP, 2)
 
-        def regroup_wo():
-            nc.scalar.copy(
-                out=wo_grouped[:].bitcast(F32).rearrange("p (c u) -> p c u", u=PAIR),
-                in_=wo_bank[0][:].rearrange("p u c -> p c u"),
-            )
+        def step_of_output(first, count):
+            return first + count + 7 + OUT_LATE.get(first // GROUP, 2 * is_spread(first + count - 1))
+
+        def transpose_wo(spread):
+            if spread:
+                wo_ps = psum.tile([P, PACK, C], BF16, tag="rows", bufs=ROW_BANKS)
+                for j in range(PACK):
+                    nc.tensor.transpose(
+                        out=wo_ps[:, j, :], in_=wo_sb[:, j * P : (j + 1) * P], identity=ident_bf16[:]
+                    )
+            else:
+                wo_ps = psum.tile([P, PAIR, C], F32, tag="rows", bufs=ROW_BANKS)
+                for u in range(PAIR):
+                    nc.tensor.transpose(
+                        out=wo_ps[:, u, :], in_=wo_sb[:].bitcast(F32)[:, u * P : (u + 1) * P], identity=ident_f32[:]
+                    )
+            wo_bank[spread] = wo_ps
+
+        def regroup_wo(spread):
+            half = wo_grouped[:, spread * C * PACK : (spread + 1) * C * PACK]
+            if spread:
+                nc.scalar.copy(
+                    out=half.rearrange("p (c j) -> p c j", j=PACK), in_=wo_bank[spread][:].rearrange("p j c -> p c j")
+                )
+            else:
+                nc.scalar.copy(
+                    out=half.bitcast(F32).rearrange("p (c u) -> p c u", u=PAIR),
+                    in_=wo_bank[spread][:].rearrange("p u c -> p c u"),
+                )
 
         def quantise_wo_and_widen_gamma():
             nc.vector.quantize_mx(out=wo_words[:].bitcast(FP8X4), scales=wo_plane[:], in_=wo_grouped[:])
@@ -162,10 +183,10 @@ def tile_selfattention_pb_t_kernel(tc, q, k, v, Wo, gamma, x, out):
                 )
             q_bank[(grp, i)] = q_ps
 
-        def copy_q(grp, i=0, count=GROUP):
+        def copy_q(grp, copy_out, i=0, count=GROUP):
             if i == 0:
                 q_cols[grp] = work.tile([P, GROUP * P], BF16, name="q_t")
-            nc.vector.tensor_copy(out=q_cols[grp][:, i * P : (i + count) * P], in_=q_bank[(grp, i)][:])
+            copy_out(out=q_cols[grp][:, i * P : (i + count) * P], in_=q_bank[(grp, i)][:])
 
         def scores(t):
             grp, i = divmod(t, GROUP)
@@ -230,32 +251,41 @@ def tile_selfattention_pb_t_kernel(tc, q, k, v, Wo, gamma, x, out):
             row_sums[first] = row_sum
 
         def reciprocal_sums(first, count):
-            one_over = work.tile([P, count], F32, name="one_over%d" % count)
-            nc.vector.reciprocal(out=one_over[:], in_=row_sums[first][:])
+            grp, j = divmod(first, GROUP)
+            one_over = recip_cols[grp % 4]
+            nc.vector.reciprocal(out=one_over[:, j : j + count], in_=row_sums[first][:])
             for i in range(count):
-                recip[first + i] = one_over[:, i : i + 1]
+                recip[first + i] = one_over[:, j + i : j + i + 1]
+
+        def spread_reciprocals(grp):
+            row = out_cols[1][grp, N - P * SPREAD : N]
+            nc.sync.dma_start(out=row.rearrange("(q e) -> q e", e=SPREAD), in_=recip_cols[grp % 4][:])
+            recip_row = work.tile([P, P * SPREAD], F32)
+            nc.sync.dma_start(out=recip_row[:], in_=row.partition_broadcast(P))
+            recip_rows[grp] = recip_row
 
         def transpose_e(t):
-            e_ps = psum.tile([P, E_PASSES, PAIR, P], F32, tag="e_t")
-            for g in range(E_PASSES):
-                for u in range(PAIR):
-                    first = (PAIR * g + u) * P
-                    nc.tensor.transpose(
-                        out=e_ps[:, g, u, :], in_=e_rows[t][:].bitcast(F32)[:, first : first + P], identity=ident_f32[:]
-                    )
+            if t == TILES - 1:
+                e_ps = psum.tile([P, E_PASSES * PAIR, P], F32, tag="scores", bufs=SCORE_BANKS)
+            else:
+                e_ps = psum.tile([P, E_PASSES * PAIR, P], F32, tag="e_t")
+            for j in range(E_PASSES * PAIR):
+                nc.tensor.transpose(
+                    out=e_ps[:, j, :], in_=e_rows[t][:].bitcast(F32)[:, j * P : (j + 1) * P], identity=ident_f32[:]
+                )
             e_bank[t] = e_ps
 
-        def regroup_e(t, copy_out):
+        def regroup_e(t):
             e_group = work.tile([P, E_PASSES * P * PACK], BF16, align_bytes=64)
-            copy_out(
+            nc.scalar.copy(
                 out=e_group[:].bitcast(F32).rearrange("p (g n u) -> p g n u", g=E_PASSES, u=PAIR),
-                in_=e_bank[t][:].rearrange("p g u n -> p g n u"),
+                in_=e_bank[t][:].rearrange("p (g u) n -> p g n u", u=PAIR),
             )
             e_grouped[t] = e_group
 
         def quantise_e(t):
-            e_word = work.tile([P, E_PASSES * P], U32, align_bytes=64, bufs=4)
-            e_scale = work.tile([P, E_PASSES * P], U8, align_bytes=64, bufs=4)
+            e_word = work.tile([P, E_PASSES * P], U32, align_bytes=64, bufs=11)
+            e_scale = work.tile([P, E_PASSES * P], U8, align_bytes=64, bufs=11)
             nc.vector.quantize_mx(out=e_word[:].bitcast(FP8X4), scales=e_scale[:], in_=e_grouped[t][:])
             e_words[t], e_plane[t] = e_word, e_scale
 
@@ -278,8 +308,8 @@ def tile_selfattention_pb_t_kernel(tc, q, k, v, Wo, gamma, x, out):
 
         def quantise_last_e(g):
             if g == 0:
-                e_words[LAST] = work.tile([P, E_PASSES * P], U32, name="e_word", align_bytes=64, bufs=4)
-                e_plane[LAST] = work.tile([P, E_PASSES * P], U8, name="e_scale", align_bytes=64, bufs=4)
+                e_words[LAST] = work.tile([P, E_PASSES * P], U32, name="e_word", align_bytes=64, bufs=11)
+                e_plane[LAST] = work.tile([P, E_PASSES * P], U8, name="e_scale", align_bytes=64, bufs=11)
             cols = slice(g * P, (g + 1) * P)
             nc.vector.quantize_mx(
                 out=e_words[LAST][:, cols].bitcast(FP8X4), scales=e_plane[LAST][:, cols], in_=e_grouped[(LAST, g)][:]
@@ -299,6 +329,36 @@ def tile_selfattention_pb_t_kernel(tc, q, k, v, Wo, gamma, x, out):
                     stop=(g == E_PASSES - 1),
                 )
             o_row_bank[t] = o_ps
+
+        def attend_spread(t):
+            b = t // TILES_PER_BATCH
+            o_ps = psum.tile([P, PACK, P], F32, tag="rows", bufs=ROW_BANKS)
+            for j in range(PACK):
+                for g in range(E_PASSES):
+                    first = g * DV + j * P
+                    nc.tensor.matmul_mx(
+                        out=o_ps[:, j, :],
+                        lhsT=v_words[b][:, first : first + P].bitcast(FP8X4),
+                        lhsT_scale=v_plane[b][:, first : first + P],
+                        rhs=e_words[t][:, g * P : (g + 1) * P].bitcast(FP8X4),
+                        rhs_scale=e_plane[t][:, g * P : (g + 1) * P],
+                        start=(g == 0),
+                        stop=(g == E_PASSES - 1),
+                    )
+            o_spread_bank[t] = o_ps
+
+        def divide_spread(t):
+            grp, i = divmod(t, GROUP)
+            o_tile = work.tile([P, P, PACK], BF16, name="o_spread", align_bytes=64)
+            nc.vector.tensor_tensor(
+                out=o_tile[:],
+                in0=o_spread_bank[t][:].rearrange("p j n -> p n j"),
+                in1=recip_rows[grp][:]
+                .rearrange("p (n e) -> p n e", e=SPREAD)[:, :, i : i + 1]
+                .to_broadcast([P, P, PACK]),
+                op=ALU.mult,
+            )
+            o_grouped[t] = o_tile
 
         def divide_o(t, on_vector):
             o_tile = work.tile([P, DV], BF16)
@@ -332,29 +392,39 @@ def tile_selfattention_pb_t_kernel(tc, q, k, v, Wo, gamma, x, out):
         def quantise_o(t):
             grp, i = divmod(t, GROUP)
             if i == 0:
-                o_words[grp] = work.tile([P, BANK], U32, name="o_word", align_bytes=64, bufs=2)
-                o_plane[grp] = work.tile([P, BANK], U8, name="o_scale", align_bytes=64, bufs=2)
+                o_words[grp] = work.tile([P, BANK], U32, name="o_word", align_bytes=64, bufs=4)
+                o_plane[grp] = work.tile([P, BANK], U8, name="o_scale", align_bytes=64, bufs=4)
             nc.vector.quantize_mx(
                 out=o_words[grp][:, i * P : (i + 1) * P].bitcast(FP8X4),
                 scales=o_plane[grp][:, i * P : (i + 1) * P],
-                in_=o_grouped[t][:],
+                in_=o_grouped[t][:].rearrange("p n j -> p (n j)") if is_spread(t) else o_grouped[t][:],
             )
 
         def project(first, count):
             grp, i = divmod(first, GROUP)
-            if first + count + 7 >= DRAIN:
+            if step_of_output(first, count) >= DRAIN:
                 y_ps = psum.tile([P, count * P], F32, tag="scores", bufs=SCORE_BANKS)
             else:
                 y_ps = psum.tile([P, count * P], F32, tag="rows", bufs=ROW_BANKS)
-            nc.tensor.matmul_mx(
-                out=y_ps[:],
-                lhsT=wo_words[:].bitcast(FP8X4),
-                lhsT_scale=wo_plane[:],
-                rhs=o_words[grp][:, i * P : (i + count) * P].bitcast(FP8X4),
-                rhs_scale=o_plane[grp][:, i * P : (i + count) * P],
-                start=True,
-                stop=True,
-            )
+            done = 0
+            while done < count:
+                order = is_spread(first + done)
+                tiles = 1
+                while done + tiles < count and is_spread(first + done + tiles) == order:
+                    tiles += 1
+                if tiles == 3:
+                    tiles = 2
+                cols = slice((i + done) * P, (i + done + tiles) * P)
+                nc.tensor.matmul_mx(
+                    out=y_ps[:, done * P : (done + tiles) * P],
+                    lhsT=wo_words[:, order * C : (order + 1) * C].bitcast(FP8X4),
+                    lhsT_scale=wo_plane[:, order * C : (order + 1) * C],
+                    rhs=o_words[grp][:, cols].bitcast(FP8X4),
+                    rhs_scale=o_plane[grp][:, cols],
+                    start=True,
+                    stop=True,
+                )
+                done += tiles
             y_bank[first] = y_ps
 
         def finish(first, count):
@@ -370,23 +440,19 @@ def tile_selfattention_pb_t_kernel(tc, q, k, v, Wo, gamma, x, out):
                 op1=ALU.add,
             )
             nc.sync.dma_start(out=out_cols[b][:, cols], in_=result[:])
-
         def is_tile(t):
             return 0 <= t < TILES
 
-        def starts_group(t):
-            return t % GROUP == 0 and 0 <= t < TILES
+        def is_plain(t):
+            return is_tile(t) and not is_spread(t)
 
         def is_chunk(c):
             return 0 <= c < V_CHUNKS
 
-        def regroup_e_on_vector(t):
-            return t % VECTOR_EVERY == VECTOR_TURN and GROUP < t < DRAIN
-
         transpose_q(0, 0, 1, "e_t", 1)
-        copy_q(0, 0, 1)
+        copy_q(0, nc.vector.tensor_copy, 0, 1)
         transpose_q(0, 1, GROUP - 1)
-        copy_q(0, 1, GROUP - 1)
+        copy_q(0, nc.vector.tensor_copy, 1, GROUP - 1)
         scores(0)
         half_maxima(0)
         negated_maximum(0)
@@ -406,84 +472,78 @@ def tile_selfattention_pb_t_kernel(tc, q, k, v, Wo, gamma, x, out):
         transpose_q(1)
         quantise_v(0, 2)
 
-        for step in range(1, TILES + 9):
-            draining = step >= DRAIN
-            if step == 4:
-                transpose_wo()
-            for t in range(step - 4 + (step > DRAIN), step - 3 + draining):
-                if is_tile(t):
-                    attend(t)
-            if is_tile(step):
-                exponentials(step)
-            if is_tile(step - 1) and step - 1 < LAST and not regroup_e_on_vector(step - 1):
-                regroup_e(step - 1, nc.scalar.copy)
-            if step == LAST + 1:
-                regroup_last_e(1, nc.scalar.copy)
-            if step == 4:
-                regroup_wo()
-            if step == 1:
-                regroup_v(0, 1, nc.scalar.copy)
 
-            if is_tile(step - 4) and step - 4 in V_DIVIDES:
-                divide_o(step - 4, True)
-            if step == LAST + 1:
-                regroup_last_e(0, nc.vector.tensor_copy)
-            for first, count in RECIPROCALS:
-                if step == first + count:
-                    add_half_sums(first, count)
+        for step in range(1, TILES + 9):
+            if step == 1:
+                regroup_v(0, 3, nc.vector.tensor_copy)
             if is_tile(step + 1):
                 half_maxima(step + 1)
             for first, count in RECIPROCALS:
                 if step == first + count:
                     reciprocal_sums(first, count)
-            if is_tile(step - 6) and step - 6 not in S_REGROUPS:
-                regroup_o(step - 6, nc.vector.tensor_copy)
-            if step == 1:
-                copy_q(1)
-            if is_tile(step - 2) and step - 2 < LAST:
-                quantise_e(step - 2)
-            if step == LAST + 1:
-                quantise_last_e(0)
-                quantise_last_e(1)
-            if step == 1:
-                regroup_v(0, 3, nc.vector.tensor_copy)
+            if is_tile(step):
+                exponentials(step)
             if step == 2:
-                quantise_v(0, 1)
-            if step == 3:
                 quantise_v(0, 3)
             if is_tile(step + 1):
                 negated_maximum(step + 1)
-            if is_tile(step - 1) and regroup_e_on_vector(step - 1):
-                regroup_e(step - 1, nc.vector.tensor_copy)
-            if is_tile(step - 7):
-                quantise_o(step - 7)
-            for grp in range(TILES // GROUP):
-                if step == grp * GROUP - 6:
-                    copy_q(grp)
-            for first, count in OUTPUTS:
-                if step == first + count + 8:
-                    finish(first, count)
+            if is_spread(step - 8):
+                attend_spread(step - 8)
+            for t in range(step - 4 + (step > DRAIN), step - 3 + (step >= DRAIN)):
+                if is_plain(t):
+                    attend(t)
+            if is_tile(step - 1) and step - 1 < LAST:
+                regroup_e(step - 1)
+            if step - 1 == LAST:
+                regroup_last_e(1, nc.scalar.copy)
+            if is_plain(step - 4) and step - 4 not in V_DIVIDES:
+                divide_o(step - 4, False)
+            if is_spread(step - 9):
+                quantise_o(step - 9)
+            if is_plain(step - 6) and step - 6 < S_REGROUPS:
+                regroup_o(step - 6, nc.vector.tensor_copy)
+            if is_tile(step - 2) and step - 2 < LAST:
+                quantise_e(step - 2)
+            if step == 1:
+                regroup_v(0, 1, nc.scalar.copy)
             if is_chunk(step - 2):
                 regroup_v(1, step - 2, nc.vector.tensor_copy)
-            if is_chunk(step - 3):
-                quantise_v(1, step - 3)
-            if step == 5:
-                quantise_wo_and_widen_gamma()
-
-            if is_tile(step - 4) and step - 4 not in V_DIVIDES:
-                divide_o(step - 4, False)
-            if is_tile(step - 6) and step - 6 in S_REGROUPS:
-                regroup_o(step - 6, nc.scalar.copy)
+            if step in (2, 3):
+                regroup_wo(step - 2)
             for first, count in OUTPUTS:
-                if step == first + count + 7:
+                if step == step_of_output(first, count):
                     project(first, count)
             if is_tile(step + 2):
                 scores(step + 2)
-            for grp in range(TILES // GROUP):
-                if step == grp * GROUP - 7:
-                    transpose_q(grp)
-            if is_tile(step - 5):
+            if step in (1, 2):
+                transpose_wo(step - 1)
+            if step - 4 in V_DIVIDES:
+                divide_o(step - 4, True)
+            if is_plain(step - 6) and step - 6 >= S_REGROUPS:
+                regroup_o(step - 6, nc.scalar.copy)
+            if step - 1 == LAST:
+                regroup_last_e(0, nc.vector.tensor_copy)
+            if is_plain(step - 7):
+                quantise_o(step - 7)
+            if is_plain(step - 5):
                 transpose_o(step - 5)
+            if is_chunk(step - 6):
+                quantise_v(1, step - 6)
+            if is_spread(step - 8):
+                divide_spread(step - 8)
+            for grp in range(MIXED):
+                if step == grp * GROUP + 5:
+                    spread_reciprocals(grp)
+            if step == 1:
+                copy_q(1, nc.vector.tensor_copy)
+            for first, count in RECIPROCALS:
+                if step == first + count - 1:
+                    add_half_sums(first, count)
+            for grp in range(2, TILES // GROUP):
+                if step == grp * GROUP - 6:
+                    transpose_q(grp)
+            if step == 2:
+                quantise_v(0, 1)
             if is_tile(step) and step < LAST:
                 transpose_e(step)
             if step == LAST:
@@ -491,3 +551,14 @@ def tile_selfattention_pb_t_kernel(tc, q, k, v, Wo, gamma, x, out):
                     transpose_last_e(g)
             if is_chunk(step - 1):
                 transpose_v(1, step - 1, "o_t", 1)
+            if step - 1 == LAST:
+                for g in range(E_PASSES):
+                    quantise_last_e(g)
+            for grp in range(2, TILES // GROUP):
+                if step == grp * GROUP - 5:
+                    copy_q(grp, nc.scalar.copy)
+            for first, count in OUTPUTS:
+                if step == step_of_output(first, count):
+                    finish(first, count)
+            if step == 5:
+                quantise_wo_and_widen_gamma()

from contextlib import ExitStack

import concourse.mybir as mybir
from concourse.masks import make_identity

BF16 = mybir.dt.bfloat16
F32 = mybir.dt.float32
U32 = mybir.dt.uint32
U8 = mybir.dt.uint8
FP8X4 = mybir.dt.float8_e4m3fn_x4
ALU = mybir.AluOpType
ACT = mybir.ActivationFunctionType
ALONG_FREE = mybir.AxisListType.X

B, N, M, D, DV, C = 2, 4096, 1024, 128, 512, 128
FLOPS = 2 * B * (N * D * M + DV * M * N + C * DV * N)

P = 128
PACK = 4
PAIR = 2
K_PASS = P * PACK
BANK = 512
HALVES = M // BANK
E_PASSES = M // K_PASS
TILES_PER_BATCH = N // P
TILES = B * TILES_PER_BATCH
GROUP = BANK // P
SCORE_BANKS = 2 * HALVES
ROW_BANKS = 2
LAST = TILES - 1
V_DIVIDES = (TILES - 6, TILES - 5)
S_REGROUPS = TILES - 8
DRAIN = TILES - 3
MIXED = 13
SPREAD = 8
RECIPROCALS = [(t, GROUP) for t in range(0, TILES - GROUP, GROUP)] + [(TILES - GROUP, GROUP - 1), (TILES - 1, 1)]
OUTPUTS = [(t, GROUP) for t in range(0, TILES - GROUP, GROUP)] + [(TILES - 4, 2), (TILES - 2, 1), (TILES - 1, 1)]
OUT_LATE = {MIXED - 2: 1, MIXED - 1: 3}
V_CHUNKS = 4
V_CHUNK_COLS = E_PASSES * DV // V_CHUNKS


def tile_selfattention_pb_t_kernel(tc, q, k, v, Wo, gamma, x, out):
    nc = tc.nc
    with ExitStack() as ctx:
        ctx.enter_context(tc.manual_schedule())
        keep = ctx.enter_context(tc.tile_pool(name="keep", bufs=1))
        work = ctx.enter_context(tc.tile_pool(name="work", bufs=3))
        psum = ctx.enter_context(tc.psum_pool(name="psum", bufs=1))

        ident_bf16 = keep.tile([P, P], BF16)
        make_identity(nc, ident_bf16[:])
        ident_f32 = keep.tile([P, P], F32)
        make_identity(nc, ident_f32[:])

        k_sb = [keep.tile([P, M], BF16, name="k_sb%d" % b) for b in range(B)]
        q_sb = [keep.tile([P, TILES_PER_BATCH, D], BF16, name="q_sb%d" % b) for b in range(B)]
        v_sb = [keep.tile([P, (DV // P) * M], BF16, name="v_sb%d" % b) for b in range(B)]
        x_sb = [keep.tile([P, N], BF16, name="x_sb%d" % b) for b in range(B)]
        wo_sb = keep.tile([P, DV], BF16)
        gamma_bf16 = keep.tile([P, 1], BF16)
        gamma_f32 = keep.tile([P, 1], F32)

        q_rows = [q[b].rearrange("(t p) d -> p t d", p=P) for b in range(B)]
        v_rows = [v[b].rearrange("(j p) m -> p j m", p=P) for b in range(B)]
        x_cols = [x[b].rearrange("c h w -> c (h w)") for b in range(B)]
        out_cols = [out[b].rearrange("c h w -> c (h w)") for b in range(B)]

        def load_q(b, first, last):
            nc.sync.dma_start(out=q_sb[b][:, first:last, :], in_=q_rows[b][:, first:last, :])

        def load_v(b, first, last):
            nc.sync.dma_start(
                out=v_sb[b][:].rearrange("p (j m) -> p j m", m=M)[:, first:last, :], in_=v_rows[b][:, first:last, :]
            )

        load_q(0, 0, GROUP)
        nc.sync.dma_start(out=k_sb[0][:], in_=k[0])
        load_v(0, 0, 2)
        nc.sync.dma_start(out=wo_sb[:], in_=Wo)
        nc.sync.dma_start(out=gamma_bf16[:], in_=gamma.partition_broadcast(P))
        load_q(0, GROUP, 2 * GROUP)
        load_v(0, 2, 4)
        load_q(0, 2 * GROUP, 4 * GROUP)
        load_v(1, 0, 4)
        load_q(0, 4 * GROUP, TILES_PER_BATCH)
        nc.sync.dma_start(out=x_sb[0][:], in_=x_cols[0])
        nc.sync.dma_start(out=k_sb[1][:], in_=k[1])
        load_q(1, 0, TILES_PER_BATCH)
        nc.sync.dma_start(out=x_sb[1][:], in_=x_cols[1])

        v_grouped = [
            keep.tile([P, E_PASSES * DV * PACK], BF16, name="v_grouped%d" % b, align_bytes=64)
            for b in range(B)
        ]
        v_words = [keep.tile([P, E_PASSES * DV], U32, name="v_words%d" % b, align_bytes=64) for b in range(B)]
        v_plane = [keep.tile([P, E_PASSES * DV], U8, name="v_plane%d" % b, align_bytes=64) for b in range(B)]
        wo_grouped = keep.tile([P, PAIR * C * PACK], BF16, align_bytes=64)
        wo_words = keep.tile([P, PAIR * C], U32, align_bytes=64)
        wo_plane = keep.tile([P, PAIR * C], U8, align_bytes=64)
        recip_cols = [keep.tile([P, SPREAD], F32, name="recip_cols%d" % i) for i in range(4)]
        for i in range(4):
            nc.gpsimd.memset(recip_cols[i][:], 0.0)

        wo_bank, v_bank, q_bank, q_cols = {}, {}, {}, {}
        score_banks, half_max, neg_max, half_sums, row_sums, recip = {}, {}, {}, {}, {}, {}
        e_rows, e_bank, e_grouped, e_words, e_plane = {}, {}, {}, {}, {}
        recip_rows, o_spread_bank, o_spread = {}, {}, {}
        o_row_bank, o_rows, o_bank, o_grouped, o_words, o_plane, y_bank = {}, {}, {}, {}, {}, {}, {}

        def is_spread(t):
            return t in range(1, MIXED * GROUP, 2)

        def step_of_output(first, count):
            return first + count + 7 + OUT_LATE.get(first // GROUP, 2 * is_spread(first + count - 1))

        def transpose_wo(spread):
            if spread:
                wo_ps = psum.tile([P, PACK, C], BF16, tag="rows", bufs=ROW_BANKS)
                for j in range(PACK):
                    nc.tensor.transpose(
                        out=wo_ps[:, j, :], in_=wo_sb[:, j * P : (j + 1) * P], identity=ident_bf16[:]
                    )
            else:
                wo_ps = psum.tile([P, PAIR, C], F32, tag="rows", bufs=ROW_BANKS)
                for u in range(PAIR):
                    nc.tensor.transpose(
                        out=wo_ps[:, u, :], in_=wo_sb[:].bitcast(F32)[:, u * P : (u + 1) * P], identity=ident_f32[:]
                    )
            wo_bank[spread] = wo_ps

        def regroup_wo(spread):
            half = wo_grouped[:, spread * C * PACK : (spread + 1) * C * PACK]
            if spread:
                nc.scalar.copy(
                    out=half.rearrange("p (c j) -> p c j", j=PACK), in_=wo_bank[spread][:].rearrange("p j c -> p c j")
                )
            else:
                nc.scalar.copy(
                    out=half.bitcast(F32).rearrange("p (c u) -> p c u", u=PAIR),
                    in_=wo_bank[spread][:].rearrange("p u c -> p c u"),
                )

        def quantise_wo_and_widen_gamma():
            nc.vector.quantize_mx(out=wo_words[:].bitcast(FP8X4), scales=wo_plane[:], in_=wo_grouped[:])
            nc.vector.tensor_copy(out=gamma_f32[:], in_=gamma_bf16[:])

        def transpose_v(b, chunk, tag, bufs):
            g, h = divmod(chunk, PAIR)
            v_ps = psum.tile([P, PAIR, PAIR, P], F32, tag=tag, bufs=bufs)
            for j in range(PAIR):
                for u in range(PAIR):
                    first_word = (PAIR * h + j) * (M // PAIR) + (PAIR * g + u) * P
                    nc.tensor.transpose(
                        out=v_ps[:, j, u, :],
                        in_=v_sb[b][:].bitcast(F32)[:, first_word : first_word + P],
                        identity=ident_f32[:],
                    )
            v_bank[(b, chunk)] = v_ps

        def regroup_v(b, chunk, copy_out):
            copy_out(
                out=v_grouped[b][:]
                .bitcast(F32)
                .rearrange("p (ch j c u) -> p ch j c u", ch=V_CHUNKS, j=PAIR, u=PAIR)[:, chunk],
                in_=v_bank[(b, chunk)][:].rearrange("p j u c -> p j c u"),
            )

        def quantise_v(b, chunk):
            cols = slice(chunk * V_CHUNK_COLS, (chunk + 1) * V_CHUNK_COLS)
            nc.vector.quantize_mx(
                out=v_words[b][:, cols].bitcast(FP8X4),
                scales=v_plane[b][:, cols],
                in_=v_grouped[b][:, chunk * V_CHUNK_COLS * PACK : (chunk + 1) * V_CHUNK_COLS * PACK],
            )

        def transpose_q(grp, i=0, count=GROUP, tag="rows", bufs=ROW_BANKS):
            b, first = divmod(grp * GROUP + i, TILES_PER_BATCH)
            q_ps = psum.tile([P, count * P], BF16, tag=tag, bufs=bufs)
            for j in range(count):
                nc.tensor.transpose(
                    out=q_ps[:, j * P : (j + 1) * P], in_=q_sb[b][:, first + j, :], identity=ident_bf16[:]
                )
            q_bank[(grp, i)] = q_ps

        def copy_q(grp, copy_out, i=0, count=GROUP):
            if i == 0:
                q_cols[grp] = work.tile([P, GROUP * P], BF16, name="q_t")
            copy_out(out=q_cols[grp][:, i * P : (i + count) * P], in_=q_bank[(grp, i)][:])

        def scores(t):
            grp, i = divmod(t, GROUP)
            banks = []
            for h in range(HALVES):
                bank = psum.tile([P, BANK], F32, tag="scores", bufs=SCORE_BANKS)
                nc.tensor.matmul(
                    out=bank[:],
                    lhsT=q_cols[grp][:, i * P : (i + 1) * P],
                    rhs=k_sb[t // TILES_PER_BATCH][:, h * BANK : (h + 1) * BANK],
                    start=True,
                    stop=True,
                )
                banks.append(bank)
            score_banks[t] = banks

        def half_maxima(t):
            maxima = work.tile([P, HALVES], F32)
            for h in range(HALVES):
                nc.vector.tensor_reduce(
                    out=maxima[:, h : h + 1], in_=score_banks[t][h][:], axis=ALONG_FREE, op=ALU.max
                )
            half_max[t] = maxima

        def negated_maximum(t):
            minus_max = work.tile([P, 1], F32)
            nc.gpsimd.tensor_scalar(
                out=minus_max[:],
                in0=half_max[t][:, 0:1],
                scalar1=half_max[t][:, 1:2],
                scalar2=-1.0,
                op0=ALU.max,
                op1=ALU.mult,
            )
            neg_max[t] = minus_max

        def exponentials(t):
            grp, i = divmod(t, GROUP)
            if i == 0:
                half_sums[grp] = work.tile([P, GROUP, HALVES], F32, name="half_sum")
            e_tile = work.tile([P, M], BF16)
            for h in range(HALVES):
                nc.scalar.activation(
                    out=e_tile[:, h * BANK : (h + 1) * BANK],
                    in_=score_banks[t][h][:],
                    func=ACT.Exp,
                    bias=neg_max[t][:, 0:1],
                    scale=1.0,
                    accum_out=half_sums[grp][:, i, h : h + 1],
                )
            e_rows[t] = e_tile

        def add_half_sums(first, count):
            grp, i = divmod(first, GROUP)
            row_sum = work.tile([P, count], F32, name="row_sum%d" % count)
            nc.gpsimd.tensor_tensor(
                out=row_sum[:],
                in0=half_sums[grp][:, i : i + count, 0],
                in1=half_sums[grp][:, i : i + count, 1],
                op=ALU.add,
            )
            row_sums[first] = row_sum

        def reciprocal_sums(first, count):
            grp, j = divmod(first, GROUP)
            one_over = recip_cols[grp % 4]
            nc.vector.reciprocal(out=one_over[:, j : j + count], in_=row_sums[first][:])
            for i in range(count):
                recip[first + i] = one_over[:, j + i : j + i + 1]

        def spread_reciprocals(grp):
            row = out_cols[1][grp, N - P * SPREAD : N]
            nc.sync.dma_start(out=row.rearrange("(q e) -> q e", e=SPREAD), in_=recip_cols[grp % 4][:])
            recip_row = work.tile([P, P * SPREAD], F32)
            nc.sync.dma_start(out=recip_row[:], in_=row.partition_broadcast(P))
            recip_rows[grp] = recip_row

        def transpose_e(t):
            if t == TILES - 1:
                e_ps = psum.tile([P, E_PASSES * PAIR, P], F32, tag="scores", bufs=SCORE_BANKS)
            else:
                e_ps = psum.tile([P, E_PASSES * PAIR, P], F32, tag="e_t")
            for j in range(E_PASSES * PAIR):
                nc.tensor.transpose(
                    out=e_ps[:, j, :], in_=e_rows[t][:].bitcast(F32)[:, j * P : (j + 1) * P], identity=ident_f32[:]
                )
            e_bank[t] = e_ps

        def regroup_e(t):
            e_group = work.tile([P, E_PASSES * P * PACK], BF16, align_bytes=64)
            nc.scalar.copy(
                out=e_group[:].bitcast(F32).rearrange("p (g n u) -> p g n u", g=E_PASSES, u=PAIR),
                in_=e_bank[t][:].rearrange("p (g u) n -> p g n u", u=PAIR),
            )
            e_grouped[t] = e_group

        def quantise_e(t):
            e_word = work.tile([P, E_PASSES * P], U32, align_bytes=64, bufs=11)
            e_scale = work.tile([P, E_PASSES * P], U8, align_bytes=64, bufs=11)
            nc.vector.quantize_mx(out=e_word[:].bitcast(FP8X4), scales=e_scale[:], in_=e_grouped[t][:])
            e_words[t], e_plane[t] = e_word, e_scale

        def transpose_last_e(g):
            e_ps = psum.tile([P, PAIR, P], F32, tag="scores", bufs=SCORE_BANKS)
            for u in range(PAIR):
                first = (PAIR * g + u) * P
                nc.tensor.transpose(
                    out=e_ps[:, u, :], in_=e_rows[LAST][:].bitcast(F32)[:, first : first + P], identity=ident_f32[:]
                )
            e_bank[(LAST, g)] = e_ps

        def regroup_last_e(g, copy_out):
            e_group = work.tile([P, P * PACK], BF16, name="last_e_group", align_bytes=64)
            copy_out(
                out=e_group[:].bitcast(F32).rearrange("p (n u) -> p n u", u=PAIR),
                in_=e_bank[(LAST, g)][:].rearrange("p u n -> p n u"),
            )
            e_grouped[(LAST, g)] = e_group

        def quantise_last_e(g):
            if g == 0:
                e_words[LAST] = work.tile([P, E_PASSES * P], U32, name="e_word", align_bytes=64, bufs=11)
                e_plane[LAST] = work.tile([P, E_PASSES * P], U8, name="e_scale", align_bytes=64, bufs=11)
            cols = slice(g * P, (g + 1) * P)
            nc.vector.quantize_mx(
                out=e_words[LAST][:, cols].bitcast(FP8X4), scales=e_plane[LAST][:, cols], in_=e_grouped[(LAST, g)][:]
            )

        def attend(t):
            b = t // TILES_PER_BATCH
            o_ps = psum.tile([P, DV], F32, tag="rows", bufs=ROW_BANKS)
            for g in range(E_PASSES):
                nc.tensor.matmul_mx(
                    out=o_ps[:],
                    lhsT=e_words[t][:, g * P : (g + 1) * P].bitcast(FP8X4),
                    lhsT_scale=e_plane[t][:, g * P : (g + 1) * P],
                    rhs=v_words[b][:, g * DV : (g + 1) * DV].bitcast(FP8X4),
                    rhs_scale=v_plane[b][:, g * DV : (g + 1) * DV],
                    start=(g == 0),
                    stop=(g == E_PASSES - 1),
                )
            o_row_bank[t] = o_ps

        def attend_spread(t):
            b = t // TILES_PER_BATCH
            o_ps = psum.tile([P, PACK, P], F32, tag="rows", bufs=ROW_BANKS)
            for j in range(PACK):
                for g in range(E_PASSES):
                    first = g * DV + j * P
                    nc.tensor.matmul_mx(
                        out=o_ps[:, j, :],
                        lhsT=v_words[b][:, first : first + P].bitcast(FP8X4),
                        lhsT_scale=v_plane[b][:, first : first + P],
                        rhs=e_words[t][:, g * P : (g + 1) * P].bitcast(FP8X4),
                        rhs_scale=e_plane[t][:, g * P : (g + 1) * P],
                        start=(g == 0),
                        stop=(g == E_PASSES - 1),
                    )
            o_spread_bank[t] = o_ps

        def divide_spread(t):
            grp, i = divmod(t, GROUP)
            o_tile = work.tile([P, P, PACK], BF16, name="o_spread", align_bytes=64)
            nc.vector.tensor_tensor(
                out=o_tile[:],
                in0=o_spread_bank[t][:].rearrange("p j n -> p n j"),
                in1=recip_rows[grp][:]
                .rearrange("p (n e) -> p n e", e=SPREAD)[:, :, i : i + 1]
                .to_broadcast([P, P, PACK]),
                op=ALU.mult,
            )
            o_grouped[t] = o_tile

        def divide_o(t, on_vector):
            o_tile = work.tile([P, DV], BF16)
            if on_vector:
                nc.vector.tensor_scalar(
                    out=o_tile[:], in0=o_row_bank[t][:], scalar1=recip[t], scalar2=None, op0=ALU.mult
                )
            else:
                nc.scalar.activation(out=o_tile[:], in_=o_row_bank[t][:], func=ACT.Copy, scale=recip[t])
            o_rows[t] = o_tile

        def transpose_o(t):
            if t >= TILES - 8 and t % 2:
                o_ps = psum.tile([P, PAIR, P], F32, tag="scores", bufs=SCORE_BANKS)
            else:
                o_ps = psum.tile([P, PAIR, P], F32, tag="o_t")
            for u in range(PAIR):
                nc.tensor.transpose(
                    out=o_ps[:, u, :], in_=o_rows[t][:].bitcast(F32)[:, u * P : (u + 1) * P], identity=ident_f32[:]
                )
            o_bank[t] = o_ps

        def regroup_o(t, copy_out):
            o_group = work.tile([P, P * PACK], BF16, align_bytes=64)
            copy_out(
                out=o_group[:].bitcast(F32).rearrange("p (n u) -> p n u", u=PAIR),
                in_=o_bank[t][:].rearrange("p u n -> p n u"),
            )
            o_grouped[t] = o_group

        def quantise_o(t):
            grp, i = divmod(t, GROUP)
            if i == 0:
                o_words[grp] = work.tile([P, BANK], U32, name="o_word", align_bytes=64, bufs=4)
                o_plane[grp] = work.tile([P, BANK], U8, name="o_scale", align_bytes=64, bufs=4)
            nc.vector.quantize_mx(
                out=o_words[grp][:, i * P : (i + 1) * P].bitcast(FP8X4),
                scales=o_plane[grp][:, i * P : (i + 1) * P],
                in_=o_grouped[t][:].rearrange("p n j -> p (n j)") if is_spread(t) else o_grouped[t][:],
            )

        def project(first, count):
            grp, i = divmod(first, GROUP)
            if step_of_output(first, count) >= DRAIN:
                y_ps = psum.tile([P, count * P], F32, tag="scores", bufs=SCORE_BANKS)
            else:
                y_ps = psum.tile([P, count * P], F32, tag="rows", bufs=ROW_BANKS)
            done = 0
            while done < count:
                order = is_spread(first + done)
                tiles = 1
                while done + tiles < count and is_spread(first + done + tiles) == order:
                    tiles += 1
                if tiles == 3:
                    tiles = 2
                cols = slice((i + done) * P, (i + done + tiles) * P)
                nc.tensor.matmul_mx(
                    out=y_ps[:, done * P : (done + tiles) * P],
                    lhsT=wo_words[:, order * C : (order + 1) * C].bitcast(FP8X4),
                    lhsT_scale=wo_plane[:, order * C : (order + 1) * C],
                    rhs=o_words[grp][:, cols].bitcast(FP8X4),
                    rhs_scale=o_plane[grp][:, cols],
                    start=True,
                    stop=True,
                )
                done += tiles
            y_bank[first] = y_ps

        def finish(first, count):
            b, i = divmod(first, TILES_PER_BATCH)
            cols = slice(i * P, (i + count) * P)
            result = work.tile([P, count * P], F32, name="result%d" % count)
            nc.vector.scalar_tensor_tensor(
                out=result[:],
                in0=y_bank[first][:],
                scalar=gamma_f32[:, 0:1],
                in1=x_sb[b][:, cols],
                op0=ALU.mult,
                op1=ALU.add,
            )
            nc.sync.dma_start(out=out_cols[b][:, cols], in_=result[:])
        def is_tile(t):
            return 0 <= t < TILES

        def is_plain(t):
            return is_tile(t) and not is_spread(t)

        def is_chunk(c):
            return 0 <= c < V_CHUNKS

        transpose_q(0, 0, 1, "e_t", 1)
        copy_q(0, nc.vector.tensor_copy, 0, 1)
        transpose_q(0, 1, GROUP - 1)
        copy_q(0, nc.vector.tensor_copy, 1, GROUP - 1)
        scores(0)
        half_maxima(0)
        negated_maximum(0)
        scores(1)
        half_maxima(1)
        negated_maximum(1)
        transpose_v(0, 0, "o_t", 1)
        regroup_v(0, 0, nc.scalar.copy)
        exponentials(0)
        transpose_v(0, 2, "e_t", 1)
        regroup_v(0, 2, nc.vector.tensor_copy)
        transpose_v(0, 1, "o_t", 1)
        transpose_v(0, 3, "rows", ROW_BANKS)
        quantise_v(0, 0)
        scores(2)
        transpose_e(0)
        transpose_q(1)
        quantise_v(0, 2)


        for step in range(1, TILES + 9):
            if step == 1:
                regroup_v(0, 3, nc.vector.tensor_copy)
            if is_tile(step + 1):
                half_maxima(step + 1)
            for first, count in RECIPROCALS:
                if step == first + count:
                    reciprocal_sums(first, count)
            if is_tile(step):
                exponentials(step)
            if step == 2:
                quantise_v(0, 3)
            if is_tile(step + 1):
                negated_maximum(step + 1)
            if is_spread(step - 8):
                attend_spread(step - 8)
            for t in range(step - 4 + (step > DRAIN), step - 3 + (step >= DRAIN)):
                if is_plain(t):
                    attend(t)
            if is_tile(step - 1) and step - 1 < LAST:
                regroup_e(step - 1)
            if step - 1 == LAST:
                regroup_last_e(1, nc.scalar.copy)
            if is_plain(step - 4) and step - 4 not in V_DIVIDES:
                divide_o(step - 4, False)
            if is_spread(step - 9):
                quantise_o(step - 9)
            if is_plain(step - 6) and step - 6 < S_REGROUPS:
                regroup_o(step - 6, nc.vector.tensor_copy)
            if is_tile(step - 2) and step - 2 < LAST:
                quantise_e(step - 2)
            if step == 1:
                regroup_v(0, 1, nc.scalar.copy)
            if is_chunk(step - 2):
                regroup_v(1, step - 2, nc.vector.tensor_copy)
            if step in (2, 3):
                regroup_wo(step - 2)
            for first, count in OUTPUTS:
                if step == step_of_output(first, count):
                    project(first, count)
            if is_tile(step + 2):
                scores(step + 2)
            if step in (1, 2):
                transpose_wo(step - 1)
            if step - 4 in V_DIVIDES:
                divide_o(step - 4, True)
            if is_plain(step - 6) and step - 6 >= S_REGROUPS:
                regroup_o(step - 6, nc.scalar.copy)
            if step - 1 == LAST:
                regroup_last_e(0, nc.vector.tensor_copy)
            if is_plain(step - 7):
                quantise_o(step - 7)
            if is_plain(step - 5):
                transpose_o(step - 5)
            if is_chunk(step - 6):
                quantise_v(1, step - 6)
            if is_spread(step - 8):
                divide_spread(step - 8)
            for grp in range(MIXED):
                if step == grp * GROUP + 5:
                    spread_reciprocals(grp)
            if step == 1:
                copy_q(1, nc.vector.tensor_copy)
            for first, count in RECIPROCALS:
                if step == first + count - 1:
                    add_half_sums(first, count)
            for grp in range(2, TILES // GROUP):
                if step == grp * GROUP - 6:
                    transpose_q(grp)
            if step == 2:
                quantise_v(0, 1)
            if is_tile(step) and step < LAST:
                transpose_e(step)
            if step == LAST:
                for g in range(E_PASSES):
                    transpose_last_e(g)
            if is_chunk(step - 1):
                transpose_v(1, step - 1, "o_t", 1)
            if step - 1 == LAST:
                for g in range(E_PASSES):
                    quantise_last_e(g)
            for grp in range(2, TILES // GROUP):
                if step == grp * GROUP - 5:
                    copy_q(grp, nc.scalar.copy)
            for first, count in OUTPUTS:
                if step == step_of_output(first, count):
                    finish(first, count)
            if step == 5:
                quantise_wo_and_widen_gamma()
